import numpy as np
import ml_dtypes


def mxq(x, axis, fmt="e4m3"):
    dtype, down = {"e4m3": (ml_dtypes.float8_e4m3fn, 7), "e5m2": (ml_dtypes.float8_e5m2, 14)}[fmt]
    v = np.moveaxis(np.asarray(x, np.float32).astype(ml_dtypes.bfloat16).astype(np.float64), axis, -1)
    blocks = v.reshape(v.shape[:-1] + (-1, 32))
    amax = np.abs(blocks).max(-1, keepdims=True)
    byte = np.maximum(np.where(amax > 0, np.frexp(amax)[1] - 1 + 127, 0) - down, 1)
    scale = np.exp2(byte - 127.0)
    codes = (blocks / scale).astype(np.float32).astype(dtype).astype(np.float64)
    return np.moveaxis((codes * scale).reshape(v.shape), -1, axis)


WIDE = False


def mx_kscale(k):
    if not WIDE:
        return np.ones(k)
    levels = np.array([10, -10, 5, -5, 0])
    a = np.random.permutation(np.resize(levels, k // 512 * 4)).reshape(k // 512, 4)
    idx = np.arange(k)
    return np.exp2(a[idx // 512, idx % 128 // 32])


BF16 = ml_dtypes.bfloat16


def bf(x):
    return np.asarray(x, np.float32).astype(BF16)


def f64(x):
    return np.asarray(x).astype(np.float64)


B, F, D, HALF, OUT = 512, 4, 32, 128, 128
CL = HALF + HALF
FINAL = HALF + HALF + CL


def cin_layer(x0, h, w, b):
    n, nf, nd = x0.shape
    ng, no = h.shape[1], w.shape[0]
    p = (x0.transpose(0, 2, 1)[:, :, :, None] * h.transpose(0, 2, 1)[:, :, None, :]).reshape(n * nd, nf * ng)
    z = (mxq(p, 1, "e4m3") @ mxq(w.reshape(no, nf * ng).T, 0, "e4m3")) + b
    return np.maximum(z, 0.0).reshape(n, nd, no).transpose(0, 2, 1)


def setup_inputs():
    s = mx_kscale(F * HALF).reshape(F, HALF)
    u, t = s[:, 0], s[0]
    v = mx_kscale(FINAL)
    return {"x": bf(np.random.standard_normal((B, F, D)) * u[None, :, None]),
            "x1": bf(np.maximum(np.random.standard_normal((B, HALF, D)), 0.0) * 0.75 * v[:HALF][None, :, None]),
            "x2": bf(np.maximum(np.random.standard_normal((B, HALF, D)), 0.0) * 0.75 * v[HALF:CL][None, :, None]),
            "h2": bf(np.maximum(np.random.standard_normal((B, HALF, D)), 0.0) * 0.75 * t[None, :, None]),
            "w3": bf(np.random.standard_normal((CL, F, HALF)) * 1.25 / np.sqrt(F * HALF) * v[CL:][:, None, None] / (u[:, None] * t[None, :])),
            "b3": bf(np.random.standard_normal(CL) * 0.3 * v[CL:]),
            "out_w": bf(np.random.standard_normal((FINAL, OUT)) * 6.0 / (D * np.sqrt(FINAL)) / v[:, None]),
            "out_b": bf(np.random.standard_normal(OUT) * 0.5)}


def reference(x, x1, x2, h2, w3, b3, out_w, out_b):
    y3 = cin_layer(f64(x), f64(h2), f64(w3), f64(b3))
    pooled = np.concatenate([f64(x1), f64(x2), y3], axis=1).sum(axis=2)
    return (mxq(pooled, 1, "e4m3") @ mxq(f64(out_w), 0, "e4m3")) + f64(out_b)

@@ -1,0 +1,320 @@
+from contextlib import ExitStack
+
+import concourse.mybir as mybir
+from concourse.masks import make_identity
+
+FLOPS = 2 * 16384 * 512 * 256 + 2 * 512 * 512 * 128
+
+F32 = mybir.dt.float32
+BF16 = mybir.dt.bfloat16
+U32 = mybir.dt.uint32
+U8 = mybir.dt.uint8
+FP8X4 = mybir.dt.float8_e4m3fn_x4
+ALU = mybir.AluOpType
+ACT = mybir.ActivationFunctionType
+AX = mybir.AxisListType
+
+P = 128
+NQ = 4
+NCT = 32
+V_CT = (1, 3, 5, 7)
+V_H = 1
+
+
+def tile_cin_pb_t_kernel(tc, x, x1, x2, h2, w3, b3, out_w, out_b, out):
+    nc = tc.nc
+    with ExitStack() as ctx:
+        const = ctx.enter_context(tc.tile_pool(name="const", bufs=1))
+        hd_pool = ctx.enter_context(tc.tile_pool(name="hdp", bufs=3))
+        p_pool = ctx.enter_context(tc.tile_pool(name="pp", bufs=3))
+        y_pool = ctx.enter_context(tc.tile_pool(name="yp", bufs=4))
+        av_pool = ctx.enter_context(tc.tile_pool(name="avp", bufs=2))
+        g_pool = ctx.enter_context(tc.tile_pool(name="gp", bufs=2))
+        a4_pool = ctx.enter_context(tc.tile_pool(name="a4p", bufs=8))
+        s2_pool = ctx.enter_context(tc.tile_pool(name="s2p", bufs=2))
+        ps_xb = ctx.enter_context(tc.psum_pool(name="psxb", bufs=4))
+        ps_z = ctx.enter_context(tc.psum_pool(name="psz", bufs=2))
+        ps_h = ctx.enter_context(tc.psum_pool(name="psh", bufs=1))
+        ps_acc = ctx.enter_context(tc.psum_pool(name="psacc", bufs=1))
+        ctx.enter_context(tc.manual_schedule())
+
+        x_sb = const.tile([P, NQ, 128], BF16, name="x_sb")
+        nc.sync.dma_start(out=x_sb[:], in_=x.rearrange("(q p) f d -> p q (f d)", p=P))
+        w3_sb = const.tile([P, 2, 512], BF16, name="w3_sb")
+        nc.sync.dma_start(out=w3_sb[:], in_=w3.rearrange("(h p) f g -> p h (f g)", p=P))
+        b3_bf = const.tile([P, 2], BF16, name="b3_bf")
+        with nc.allow_non_contiguous_dma(reason="256 bias values, one per partition and half"):
+            nc.scalar.dma_start(out=b3_bf[:], in_=b3.rearrange("(h p) -> p h", p=P))
+        ow_sb = const.tile([P, 4, 128], BF16, name="ow_sb")
+        nc.scalar.dma_start(out=ow_sb[:], in_=out_w.rearrange("(t p) j -> p t j", p=P))
+        outb = const.tile([P, 128], BF16, name="outb")
+        nc.scalar.dma_start(out=outb[:], in_=out_b.partition_broadcast(P))
+        h2_sb = []
+        x12_sb = []
+        for q in range(NQ):
+            rows = slice(q * P, (q + 1) * P)
+            h2_t = const.tile([P, 4096], BF16, name="h2_sb%d" % q)
+            nc.sync.dma_start(out=h2_t[:], in_=h2[rows].rearrange("n g d -> n (g d)"))
+            h2_sb.append(h2_t)
+            x1_t = const.tile([P, 4096], BF16, name="x1_sb%d" % q)
+            nc.sync.dma_start(out=x1_t[:], in_=x1[rows].rearrange("n g d -> n (g d)"))
+            x2_t = const.tile([P, 4096], BF16, name="x2_sb%d" % q)
+            nc.sync.dma_start(out=x2_t[:], in_=x2[rows].rearrange("n g d -> n (g d)"))
+            x12_sb.append((x1_t, x2_t))
+
+        ident_f = const.tile([P, P], F32, name="ident_f")
+        make_identity(nc, ident_f[:])
+        ident_b = const.tile([P, P], BF16, name="ident_b")
+        make_identity(nc, ident_b[:])
+
+        xw = const.tile([P, 512], BF16, name="xw")
+        nc.vector.tensor_copy(
+            out=xw[:].rearrange("p (q d f) -> p q d f", q=NQ, f=4),
+            in_=x_sb[:].rearrange("p q (f d) -> p q d f", f=4),
+        )
+        xw_words = xw[:].bitcast(F32)
+
+        w_t = ps_z.tile([P, 1024], BF16, name="w_t", tag="z")
+        for h in range(2):
+            for f in range(4):
+                k = h * 4 + f
+                nc.tensor.transpose(w_t[:, k * P:(k + 1) * P], w3_sb[:, h, f * P:(f + 1) * P], ident_b[:])
+        w_g = const.tile([P, 1024], BF16, name="w_g", align_bytes=64)
+        nc.vector.tensor_copy(
+            out=w_g[:].rearrange("p (h o f) -> p h o f", h=2, f=4),
+            in_=w_t[:].rearrange("p (h f o) -> p h o f", h=2, f=4),
+        )
+        ow_g = const.tile([P, 512], BF16, name="ow_g", align_bytes=64)
+        nc.vector.tensor_copy(
+            out=ow_g[:].rearrange("p (j t) -> p j t", t=4),
+            in_=ow_sb[:].rearrange("p t j -> p j t"),
+        )
+        w_codes = const.tile([P, 256], U32, name="w_codes", align_bytes=64)
+        w_scales = const.tile([P, 256], U8, name="w_scales", align_bytes=64)
+        nc.vector.quantize_mx(out=w_codes[:].bitcast(FP8X4), scales=w_scales[:], in_=w_g[:])
+        ow_codes = const.tile([P, 128], U32, name="ow_codes", align_bytes=64)
+        ow_scales = const.tile([P, 128], U8, name="ow_scales", align_bytes=64)
+        nc.vector.quantize_mx(out=ow_codes[:].bitcast(FP8X4), scales=ow_scales[:], in_=ow_g[:])
+
+        b3_f = const.tile([P, 2], F32, name="b3_f")
+        nc.vector.tensor_copy(out=b3_f[:], in_=b3_bf[:])
+        b3_neg = const.tile([P, 2], F32, name="b3_neg")
+        nc.vector.tensor_scalar(out=b3_neg[:], in0=b3_bf[:], scalar1=-1.0, scalar2=None, op0=ALU.mult)
+        b3_n = const.tile([P, 2], F32, name="b3_n")
+        nc.vector.tensor_scalar(out=b3_n[:], in0=b3_bf[:], scalar1=float(len(V_CT)), scalar2=None, op0=ALU.mult)
+
+        a4 = {}
+        for q in range(NQ):
+            for t in range(2):
+                src = x12_sb[q][t][:].rearrange("p (c d) -> p c d", d=32)
+                a16 = g_pool.tile([P, 128, 16], F32, name="a16", tag="a16")
+                nc.gpsimd.tensor_tensor(out=a16[:], in0=src[:, :, 0:16], in1=src[:, :, 16:32], op=ALU.add)
+                a8 = g_pool.tile([P, 128, 8], F32, name="a8", tag="a8")
+                nc.gpsimd.tensor_tensor(out=a8[:], in0=a16[:, :, 0:8], in1=a16[:, :, 8:16], op=ALU.add)
+                a4_t = a4_pool.tile([P, 128, 4], F32, name="a4_t", tag="a4")
+                nc.gpsimd.tensor_tensor(out=a4_t[:], in0=a8[:, :, 0:4], in1=a8[:, :, 4:8], op=ALU.add)
+                a4[(q, t)] = a4_t
+
+        ht = {}
+        hd = {}
+        xbs = {}
+        pts = {}
+        cds = {}
+        zs = {}
+        ys = {}
+        avs = {}
+        accs = {}
+        pls = {}
+        st2 = {}
+
+        def t_h(u):
+            q, b = divmod(u, 4)
+            hw = h2_sb[q][:].bitcast(F32).rearrange("p (g j) -> p g j", j=16)
+            ht_t = ps_h.tile([P, 512], F32, name="ht_t", tag="ht")
+            for jj in range(4):
+                nc.tensor.transpose(ht_t[:, jj * P:(jj + 1) * P], hw[:, :, 4 * b + jj], ident_f[:])
+            ht[u] = ht_t
+
+        def hd_exit(u, e):
+            if e == 0:
+                hd[u] = hd_pool.tile([P, 8, 128, 2], BF16, name="hd_t", tag="hd")
+            src = ht[u][:].bitcast(BF16).rearrange("p (jj n e) -> p jj n e", jj=4, e=2)
+            dst = hd[u][:].rearrange("p (jj e) n u -> p jj e n u", e=2)
+            nc.scalar.copy(out=dst[:, :, e, :, :], in_=src[:, :, :, e:e + 1].to_broadcast([P, 4, 128, 2]))
+
+        def t_xb(i):
+            q, c = divmod(i, 8)
+            tiles = []
+            for s in range(2):
+                xb = ps_xb.tile([P, 512], F32, name="xb", tag="xb")
+                for fp in range(2):
+                    for dl in range(2):
+                        w = (q * 32 + 4 * c + 2 * s + dl) * 2 + fp
+                        k = fp * 2 + dl
+                        nc.tensor.transpose(
+                            xb[:, k * P:(k + 1) * P], xw_words[:, w:w + 1].to_broadcast([P, P]), ident_f[:]
+                        )
+                tiles.append(xb)
+            xbs[i] = tiles
+
+        def mult(i):
+            u = i // 2
+            pt = p_pool.tile([P, 2048], BF16, name="pt", tag="pt", align_bytes=64)
+            for s in range(2):
+                dloc = (i % 2) * 4 + 2 * s
+                in0 = hd[u][:, dloc:dloc + 2, :, :].rearrange("p d n u -> p (d n) u")
+                nc.vector.tensor_tensor(
+                    out=pt[:, s * 1024:(s + 1) * 1024].rearrange("p (c fp e) -> p c fp e", fp=2, e=2),
+                    in0=in0.unsqueeze(2).to_broadcast([P, 256, 2, 2]),
+                    in1=xbs[i][s][:].bitcast(BF16).rearrange("p (fp c e) -> p c fp e", fp=2, e=2),
+                    op=ALU.mult,
+                )
+            pts[i] = pt
+
+        def quant(i):
+            codes = p_pool.tile([P, 512], U32, name="codes", tag="codes", align_bytes=64)
+            scales = p_pool.tile([P, 512], U8, name="scales", tag="scales", align_bytes=64)
+            nc.vector.quantize_mx(out=codes[:].bitcast(FP8X4), scales=scales[:], in_=pts[i][:])
+            cds[i] = (codes, scales)
+
+        def mx(i):
+            codes, scales = cds[i]
+            for h in range(2):
+                z = ps_z.tile([P, 512], F32, name="z", tag="z")
+                nc.tensor.matmul_mx(
+                    out=z[:],
+                    lhsT=w_codes[:, h * P:(h + 1) * P].bitcast(FP8X4),
+                    lhsT_scale=w_scales[:, h * P:(h + 1) * P],
+                    rhs=codes[:].bitcast(FP8X4),
+                    rhs_scale=scales[:],
+                    start=True,
+                    stop=True,
+                )
+                zs[(i, h)] = z
+
+        def on_vector(i, h):
+            return h == V_H and (i % 8) in V_CT
+
+        def relu_s(i):
+            for h in range(2):
+                if not on_vector(i, h):
+                    y = y_pool.tile([P, 512], F32, name="y", tag="y")
+                    nc.scalar.activation(out=y[:], in_=zs[(i, h)][:], func=ACT.Relu, bias=b3_f[:, h:h + 1], scale=1.0)
+                    ys[(i, h)] = y
+
+        def relu_v(i):
+            q, c = divmod(i, 8)
+            h = V_H
+            if on_vector(i, h):
+                if c == V_CT[0]:
+                    av = av_pool.tile([P, 512], F32, name="av", tag="av")
+                    avs[q] = av
+                    nc.vector.tensor_scalar(
+                        out=av[:], in0=zs[(i, h)][:], scalar1=b3_neg[:, h:h + 1], scalar2=b3_n[:, h:h + 1],
+                        op0=ALU.max, op1=ALU.add,
+                    )
+                else:
+                    av = avs[q]
+                    nc.vector.scalar_tensor_tensor(
+                        out=av[:], in0=zs[(i, h)][:], scalar=b3_neg[:, h:h + 1], in1=av[:], op0=ALU.max, op1=ALU.add,
+                    )
+
+        def acc_t(i):
+            q, c = divmod(i, 8)
+            if c == 0:
+                accs[q] = ps_acc.tile([P, 256], F32, name="acc", tag="acc")
+            acc = accs[q]
+            todo = [(ys[(i, h)], h) for h in range(2) if not on_vector(i, h)]
+            if c == 7:
+                todo.append((avs[q], V_H))
+            for k, (src, h) in enumerate(todo):
+                for dl in range(4):
+                    nc.tensor.matmul(
+                        out=acc[:, h * P:(h + 1) * P],
+                        lhsT=src[:, dl * P:(dl + 1) * P],
+                        rhs=ident_f[:],
+                        start=(c == 0 and k == 0 and dl == 0),
+                        stop=(c == 7 and k == len(todo) - 1 and dl == 3),
+                        is_transpose=True,
+                    )
+
+        def pool12(q):
+            pl = s2_pool.tile([P, 512], BF16, name="pl", tag="pl")
+            pls[q] = pl
+            with nc.allow_low_precision(reason="float32 sum, rounded once to bfloat16 for quantize_mx"):
+                for t in range(2):
+                    nc.vector.tensor_reduce(out=pl[:, t * P:(t + 1) * P], in_=a4[(q, t)][:], axis=AX.X, op=ALU.add)
+
+        def acc_exit(q):
+            nc.vector.tensor_copy(out=pls[q][:, 256:512], in_=accs[q][:])
+
+        def s2_transpose(q):
+            pt2 = ps_z.tile([P, 512], BF16, name="pt2", tag="z")
+            for t in range(4):
+                nc.tensor.transpose(pt2[:, t * P:(t + 1) * P], pls[q][:, t * P:(t + 1) * P], ident_b[:])
+            st2[(q, "pt2")] = pt2
+
+        def s2_group(q):
+            g2 = s2_pool.tile([P, 512], BF16, name="g2", tag="g2", align_bytes=64)
+            nc.vector.tensor_copy(
+                out=g2[:].rearrange("p (n t) -> p n t", t=4),
+                in_=st2[(q, "pt2")][:].rearrange("p (t n) -> p n t", t=4),
+            )
+            st2[(q, "g2")] = g2
+
+        def s2_quant(q):
+            c2 = s2_pool.tile([P, 128], U32, name="c2", tag="c2", align_bytes=64)
+            sc2 = s2_pool.tile([P, 128], U8, name="sc2", tag="sc2", align_bytes=64)
+            nc.vector.quantize_mx(out=c2[:].bitcast(FP8X4), scales=sc2[:], in_=st2[(q, "g2")][:])
+            st2[(q, "c2")] = (c2, sc2)
+
+        def s2_mx(q):
+            c2, sc2 = st2[(q, "c2")]
+            o2 = ps_z.tile([P, 128], F32, name="o2", tag="z")
+            nc.tensor.matmul_mx(
+                out=o2[:], lhsT=c2[:].bitcast(FP8X4), lhsT_scale=sc2[:],
+                rhs=ow_codes[:].bitcast(FP8X4), rhs_scale=ow_scales[:], start=True, stop=True,
+            )
+            st2[(q, "o2")] = o2
+
+        def s2_out(q):
+            res = s2_pool.tile([P, 128], F32, name="res", tag="res")
+            nc.vector.tensor_tensor(out=res[:], in0=st2[(q, "o2")][:], in1=outb[:], op=ALU.add)
+            nc.sync.dma_start(out=out[q * P:(q + 1) * P, :], in_=res[:])
+
+        for i in range(-4, NCT + 5):
+            q9, r9 = divmod(i - 9, 8)
+            q10, r10 = divmod(i - 10, 8)
+            q11, r11 = divmod(i - 11, 8)
+            q6, r6 = divmod(i - 6, 8)
+            if i % 2 == 0 and 0 <= i // 2 + 1 < 16:
+                hd_exit(i // 2 + 1, 1)
+            if 0 <= i - 1 < NCT:
+                relu_s(i - 1)
+                relu_v(i - 1)
+            if r9 == 0 and 0 <= q9 < NQ:
+                acc_exit(q9)
+            if 0 <= i < NCT:
+                quant(i)
+            if r10 == 0 and 0 <= q10 < NQ:
+                s2_transpose(q10)
+                s2_group(q10)
+            if 0 <= i + 2 < NCT:
+                t_xb(i + 2)
+            if r11 == 0 and 0 <= q11 < NQ:
+                s2_mx(q11)
+                s2_out(q11)
+            if 0 <= i < NCT:
+                mx(i)
+            if 0 <= i - 1 < NCT:
+                acc_t(i - 1)
+            if 0 <= i + 1 < NCT:
+                mult(i + 1)
+            if r6 == 0 and 0 <= q6 < NQ:
+                pool12(q6)
+            if r10 == 0 and 0 <= q10 < NQ:
+                s2_quant(q10)
+            if i % 2 != 0 and 0 <= (i - 1) // 2 + 2 < 16:
+                hd_exit((i - 1) // 2 + 2, 0)
+            if i % 2 == 0 and 0 <= i // 2 + 2 < 16:
+                t_h(i // 2 + 2)

@@ -29,8 +29,6 @@ def tile_cin_pb_t_kernel(tc, x, x1, x2, h2, w3, b3, out_w, out_b, out):
         p_pool = ctx.enter_context(tc.tile_pool(name="pp", bufs=3))
         y_pool = ctx.enter_context(tc.tile_pool(name="yp", bufs=4))
         av_pool = ctx.enter_context(tc.tile_pool(name="avp", bufs=2))
-        g_pool = ctx.enter_context(tc.tile_pool(name="gp", bufs=2))
-        a4_pool = ctx.enter_context(tc.tile_pool(name="a4p", bufs=8))
         s2_pool = ctx.enter_context(tc.tile_pool(name="s2p", bufs=2))
         ps_xb = ctx.enter_context(tc.psum_pool(name="psxb", bufs=4))
         ps_z = ctx.enter_context(tc.psum_pool(name="psz", bufs=2))
@@ -102,18 +100,6 @@ def tile_cin_pb_t_kernel(tc, x, x1, x2, h2, w3, b3, out_w, out_b, out):
         nc.vector.tensor_scalar(out=b3_neg[:], in0=b3_bf[:], scalar1=-1.0, scalar2=None, op0=ALU.mult)
         b3_n = const.tile([P, 2], F32, name="b3_n")
         nc.vector.tensor_scalar(out=b3_n[:], in0=b3_bf[:], scalar1=float(len(V_CT)), scalar2=None, op0=ALU.mult)
-
-        a4 = {}
-        for q in range(NQ):
-            for t in range(2):
-                src = x12_sb[q][t][:].rearrange("p (c d) -> p c d", d=32)
-                a16 = g_pool.tile([P, 128, 16], F32, name="a16", tag="a16")
-                nc.gpsimd.tensor_tensor(out=a16[:], in0=src[:, :, 0:16], in1=src[:, :, 16:32], op=ALU.add)
-                a8 = g_pool.tile([P, 128, 8], F32, name="a8", tag="a8")
-                nc.gpsimd.tensor_tensor(out=a8[:], in0=a16[:, :, 0:8], in1=a16[:, :, 8:16], op=ALU.add)
-                a4_t = a4_pool.tile([P, 128, 4], F32, name="a4_t", tag="a4")
-                nc.gpsimd.tensor_tensor(out=a4_t[:], in0=a8[:, :, 0:4], in1=a8[:, :, 4:8], op=ALU.add)
-                a4[(q, t)] = a4_t
 
         ht = {}
         hd = {}
@@ -238,12 +224,17 @@ def tile_cin_pb_t_kernel(tc, x, x1, x2, h2, w3, b3, out_w, out_b, out):
                         is_transpose=True,
                     )
 
-        def pool12(q):
-            pl = s2_pool.tile([P, 512], BF16, name="pl", tag="pl")
-            pls[q] = pl
+        def pool12(i):
+            q, r = divmod(i, 8)
+            t, part = divmod(r, 4)
+            if r == 0:
+                pls[q] = s2_pool.tile([P, 512], BF16, name="pl", tag="pl")
+            src = x12_sb[q][t][:].rearrange("p (c d) -> p c d", d=32)
             with nc.allow_low_precision(reason="float32 sum, rounded once to bfloat16 for quantize_mx"):
-                for t in range(2):
-                    nc.vector.tensor_reduce(out=pl[:, t * P:(t + 1) * P], in_=a4[(q, t)][:], axis=AX.X, op=ALU.add)
+                nc.vector.tensor_reduce(
+                    out=pls[q][:, t * P + part * 32:t * P + (part + 1) * 32],
+                    in_=src[:, part * 32:(part + 1) * 32, :], axis=AX.X, op=ALU.add,
+                )
 
         def acc_exit(q):
             nc.vector.tensor_copy(out=pls[q][:, 256:512], in_=accs[q][:])
@@ -286,7 +277,6 @@ def tile_cin_pb_t_kernel(tc, x, x1, x2, h2, w3, b3, out_w, out_b, out):
             q9, r9 = divmod(i - 9, 8)
             q10, r10 = divmod(i - 10, 8)
             q11, r11 = divmod(i - 11, 8)
-            q6, r6 = divmod(i - 6, 8)
             if i % 2 == 0 and 0 <= i // 2 + 1 < 16:
                 hd_exit(i // 2 + 1, 1)
             if 0 <= i - 1 < NCT:
@@ -310,8 +300,8 @@ def tile_cin_pb_t_kernel(tc, x, x1, x2, h2, w3, b3, out_w, out_b, out):
                 acc_t(i - 1)
             if 0 <= i + 1 < NCT:
                 mult(i + 1)
-            if r6 == 0 and 0 <= q6 < NQ:
-                pool12(q6)
+            if 0 <= i < NCT:
+                pool12(i)
             if r10 == 0 and 0 <= q10 < NQ:
                 s2_quant(q10)
             if i % 2 != 0 and 0 <= (i - 1) // 2 + 2 < 16:

@@ -17,8 +17,6 @@ AX = mybir.AxisListType
 P = 128
 NQ = 4
 NCT = 32
-V_CT = (1, 3, 5, 7)
-V_H = 1
 
 
 def tile_cin_pb_t_kernel(tc, x, x1, x2, h2, w3, b3, out_w, out_b, out):
@@ -28,7 +26,6 @@ def tile_cin_pb_t_kernel(tc, x, x1, x2, h2, w3, b3, out_w, out_b, out):
         hd_pool = ctx.enter_context(tc.tile_pool(name="hdp", bufs=3))
         p_pool = ctx.enter_context(tc.tile_pool(name="pp", bufs=3))
         y_pool = ctx.enter_context(tc.tile_pool(name="yp", bufs=4))
-        av_pool = ctx.enter_context(tc.tile_pool(name="avp", bufs=2))
         s2_pool = ctx.enter_context(tc.tile_pool(name="s2p", bufs=2))
         ps_xb = ctx.enter_context(tc.psum_pool(name="psxb", bufs=4))
         ps_z = ctx.enter_context(tc.psum_pool(name="psz", bufs=2))
@@ -52,10 +49,13 @@ def tile_cin_pb_t_kernel(tc, x, x1, x2, h2, w3, b3, out_w, out_b, out):
         for q in range(NQ):
             rows = slice(q * P, (q + 1) * P)
             h2_t = const.tile([P, 4096], BF16, name="h2_sb%d" % q)
+            x1_t = const.tile([P, 4096], BF16, name="x1_sb%d" % q)
+            if q == 0:
+                nc.sync.dma_start(out=x1_t[:], in_=x1[rows].rearrange("n g d -> n (g d)"))
             nc.sync.dma_start(out=h2_t[:], in_=h2[rows].rearrange("n g d -> n (g d)"))
             h2_sb.append(h2_t)
-            x1_t = const.tile([P, 4096], BF16, name="x1_sb%d" % q)
-            nc.sync.dma_start(out=x1_t[:], in_=x1[rows].rearrange("n g d -> n (g d)"))
+            if q != 0:
+                nc.sync.dma_start(out=x1_t[:], in_=x1[rows].rearrange("n g d -> n (g d)"))
             x2_t = const.tile([P, 4096], BF16, name="x2_sb%d" % q)
             nc.sync.dma_start(out=x2_t[:], in_=x2[rows].rearrange("n g d -> n (g d)"))
             x12_sb.append((x1_t, x2_t))
@@ -95,11 +95,7 @@ def tile_cin_pb_t_kernel(tc, x, x1, x2, h2, w3, b3, out_w, out_b, out):
         nc.vector.quantize_mx(out=ow_codes[:].bitcast(FP8X4), scales=ow_scales[:], in_=ow_g[:])
 
         b3_f = const.tile([P, 2], F32, name="b3_f")
-        nc.vector.tensor_copy(out=b3_f[:], in_=b3_bf[:])
-        b3_neg = const.tile([P, 2], F32, name="b3_neg")
-        nc.vector.tensor_scalar(out=b3_neg[:], in0=b3_bf[:], scalar1=-1.0, scalar2=None, op0=ALU.mult)
-        b3_n = const.tile([P, 2], F32, name="b3_n")
-        nc.vector.tensor_scalar(out=b3_n[:], in0=b3_bf[:], scalar1=float(len(V_CT)), scalar2=None, op0=ALU.mult)
+        nc.gpsimd.tensor_copy(out=b3_f[:], in_=b3_bf[:])
 
         ht = {}
         hd = {}
@@ -108,7 +104,6 @@ def tile_cin_pb_t_kernel(tc, x, x1, x2, h2, w3, b3, out_w, out_b, out):
         cds = {}
         zs = {}
         ys = {}
-        avs = {}
         accs = {}
         pls = {}
         st2 = {}
@@ -121,12 +116,19 @@ def tile_cin_pb_t_kernel(tc, x, x1, x2, h2, w3, b3, out_w, out_b, out):
                 nc.tensor.transpose(ht_t[:, jj * P:(jj + 1) * P], hw[:, :, 4 * b + jj], ident_f[:])
             ht[u] = ht_t
 
-        def hd_exit(u, e):
-            if e == 0:
+        def hd_exit(u, part):
+            if part == 0:
                 hd[u] = hd_pool.tile([P, 8, 128, 2], BF16, name="hd_t", tag="hd")
             src = ht[u][:].bitcast(BF16).rearrange("p (jj n e) -> p jj n e", jj=4, e=2)
             dst = hd[u][:].rearrange("p (jj e) n u -> p jj e n u", e=2)
-            nc.scalar.copy(out=dst[:, :, e, :, :], in_=src[:, :, :, e:e + 1].to_broadcast([P, 4, 128, 2]))
+            if u == 0:
+                pieces = [(2 * part, 2 * part + 2, e) for e in range(2)]
+            else:
+                pieces = [(0, 4, part)]
+            for lo, hi, e in pieces:
+                nc.scalar.copy(
+                    out=dst[:, lo:hi, e, :, :], in_=src[:, lo:hi, :, e:e + 1].to_broadcast([P, hi - lo, 128, 2])
+                )
 
         def t_xb(i):
             q, c = divmod(i, 8)
@@ -178,49 +180,25 @@ def tile_cin_pb_t_kernel(tc, x, x1, x2, h2, w3, b3, out_w, out_b, out):
                 )
                 zs[(i, h)] = z
 
-        def on_vector(i, h):
-            return h == V_H and (i % 8) in V_CT
-
         def relu_s(i):
             for h in range(2):
-                if not on_vector(i, h):
-                    y = y_pool.tile([P, 512], F32, name="y", tag="y")
-                    nc.scalar.activation(out=y[:], in_=zs[(i, h)][:], func=ACT.Relu, bias=b3_f[:, h:h + 1], scale=1.0)
-                    ys[(i, h)] = y
-
-        def relu_v(i):
-            q, c = divmod(i, 8)
-            h = V_H
-            if on_vector(i, h):
-                if c == V_CT[0]:
-                    av = av_pool.tile([P, 512], F32, name="av", tag="av")
-                    avs[q] = av
-                    nc.vector.tensor_scalar(
-                        out=av[:], in0=zs[(i, h)][:], scalar1=b3_neg[:, h:h + 1], scalar2=b3_n[:, h:h + 1],
-                        op0=ALU.max, op1=ALU.add,
-                    )
-                else:
-                    av = avs[q]
-                    nc.vector.scalar_tensor_tensor(
-                        out=av[:], in0=zs[(i, h)][:], scalar=b3_neg[:, h:h + 1], in1=av[:], op0=ALU.max, op1=ALU.add,
-                    )
+                y = y_pool.tile([P, 512], F32, name="y", tag="y")
+                nc.scalar.activation(out=y[:], in_=zs[(i, h)][:], func=ACT.Relu, bias=b3_f[:, h:h + 1], scale=1.0)
+                ys[(i, h)] = y
 
         def acc_t(i):
             q, c = divmod(i, 8)
             if c == 0:
                 accs[q] = ps_acc.tile([P, 256], F32, name="acc", tag="acc")
             acc = accs[q]
-            todo = [(ys[(i, h)], h) for h in range(2) if not on_vector(i, h)]
-            if c == 7:
-                todo.append((avs[q], V_H))
-            for k, (src, h) in enumerate(todo):
+            for h in range(2):
                 for dl in range(4):
                     nc.tensor.matmul(
                         out=acc[:, h * P:(h + 1) * P],
-                        lhsT=src[:, dl * P:(dl + 1) * P],
+                        lhsT=ys[(i, h)][:, dl * P:(dl + 1) * P],
                         rhs=ident_f[:],
-                        start=(c == 0 and k == 0 and dl == 0),
-                        stop=(c == 7 and k == len(todo) - 1 and dl == 3),
+                        start=(c == 0 and h == 0 and dl == 0),
+                        stop=(c == 7 and h == 1 and dl == 3),
                         is_transpose=True,
                     )
 
@@ -237,7 +215,7 @@ def tile_cin_pb_t_kernel(tc, x, x1, x2, h2, w3, b3, out_w, out_b, out):
                 )
 
         def acc_exit(q):
-            nc.vector.tensor_copy(out=pls[q][:, 256:512], in_=accs[q][:])
+            nc.scalar.copy(out=pls[q][:, 256:512], in_=accs[q][:])
 
         def s2_transpose(q):
             pt2 = ps_z.tile([P, 512], BF16, name="pt2", tag="z")
@@ -273,23 +251,24 @@ def tile_cin_pb_t_kernel(tc, x, x1, x2, h2, w3, b3, out_w, out_b, out):
             nc.vector.tensor_tensor(out=res[:], in0=st2[(q, "o2")][:], in1=outb[:], op=ALU.add)
             nc.sync.dma_start(out=out[q * P:(q + 1) * P, :], in_=res[:])
 
-        for i in range(-4, NCT + 5):
+        t_xb(0)
+        t_xb(1)
+        for i in range(-5, NCT + 5):
             q9, r9 = divmod(i - 9, 8)
             q10, r10 = divmod(i - 10, 8)
             q11, r11 = divmod(i - 11, 8)
             if i % 2 == 0 and 0 <= i // 2 + 1 < 16:
                 hd_exit(i // 2 + 1, 1)
-            if 0 <= i - 1 < NCT:
-                relu_s(i - 1)
-                relu_v(i - 1)
             if r9 == 0 and 0 <= q9 < NQ:
                 acc_exit(q9)
+            if 0 <= i - 1 < NCT:
+                relu_s(i - 1)
             if 0 <= i < NCT:
                 quant(i)
             if r10 == 0 and 0 <= q10 < NQ:
                 s2_transpose(q10)
                 s2_group(q10)
-            if 0 <= i + 2 < NCT:
+            if 2 <= i + 2 < NCT:
                 t_xb(i + 2)
             if r11 == 0 and 0 <= q11 < NQ:
                 s2_mx(q11)
@@ -300,8 +279,8 @@ def tile_cin_pb_t_kernel(tc, x, x1, x2, h2, w3, b3, out_w, out_b, out):
                 acc_t(i - 1)
             if 0 <= i + 1 < NCT:
                 mult(i + 1)
-            if 0 <= i < NCT:
-                pool12(i)
+            if 0 <= i + 5 < NCT:
+                pool12(i + 5)
             if r10 == 0 and 0 <= q10 < NQ:
                 s2_quant(q10)
             if i % 2 != 0 and 0 <= (i - 1) // 2 + 2 < 16:

@@ -17,6 +17,10 @@ AX = mybir.AxisListType
 P = 128
 NQ = 4
 NCT = 32
+V_CT = (1, 3, 5, 7)
+V_H = 1
+V_POOL = {0: (0, 0, 32), 2: (0, 32, 64), 4: (0, 64, 96), 6: (0, 96, 128), 1: (1, 0, 16), 5: (1, 16, 32)}
+S_POOL = (8, 16, 8, 16, 8, 16, 8, 16)
 
 
 def tile_cin_pb_t_kernel(tc, x, x1, x2, h2, w3, b3, out_w, out_b, out):
@@ -26,6 +30,7 @@ def tile_cin_pb_t_kernel(tc, x, x1, x2, h2, w3, b3, out_w, out_b, out):
         hd_pool = ctx.enter_context(tc.tile_pool(name="hdp", bufs=3))
         p_pool = ctx.enter_context(tc.tile_pool(name="pp", bufs=3))
         y_pool = ctx.enter_context(tc.tile_pool(name="yp", bufs=4))
+        av_pool = ctx.enter_context(tc.tile_pool(name="avp", bufs=2))
         s2_pool = ctx.enter_context(tc.tile_pool(name="s2p", bufs=2))
         ps_xb = ctx.enter_context(tc.psum_pool(name="psxb", bufs=4))
         ps_z = ctx.enter_context(tc.psum_pool(name="psz", bufs=2))
@@ -36,7 +41,6 @@ def tile_cin_pb_t_kernel(tc, x, x1, x2, h2, w3, b3, out_w, out_b, out):
         x_sb = const.tile([P, NQ, 128], BF16, name="x_sb")
         nc.sync.dma_start(out=x_sb[:], in_=x.rearrange("(q p) f d -> p q (f d)", p=P))
         w3_sb = const.tile([P, 2, 512], BF16, name="w3_sb")
-        nc.sync.dma_start(out=w3_sb[:], in_=w3.rearrange("(h p) f g -> p h (f g)", p=P))
         b3_bf = const.tile([P, 2], BF16, name="b3_bf")
         with nc.allow_non_contiguous_dma(reason="256 bias values, one per partition and half"):
             nc.scalar.dma_start(out=b3_bf[:], in_=b3.rearrange("(h p) -> p h", p=P))
@@ -50,12 +54,11 @@ def tile_cin_pb_t_kernel(tc, x, x1, x2, h2, w3, b3, out_w, out_b, out):
             rows = slice(q * P, (q + 1) * P)
             h2_t = const.tile([P, 4096], BF16, name="h2_sb%d" % q)
             x1_t = const.tile([P, 4096], BF16, name="x1_sb%d" % q)
-            if q == 0:
-                nc.sync.dma_start(out=x1_t[:], in_=x1[rows].rearrange("n g d -> n (g d)"))
             nc.sync.dma_start(out=h2_t[:], in_=h2[rows].rearrange("n g d -> n (g d)"))
             h2_sb.append(h2_t)
-            if q != 0:
-                nc.sync.dma_start(out=x1_t[:], in_=x1[rows].rearrange("n g d -> n (g d)"))
+            if q == 0:
+                nc.sync.dma_start(out=w3_sb[:], in_=w3.rearrange("(h p) f g -> p h (f g)", p=P))
+            nc.sync.dma_start(out=x1_t[:], in_=x1[rows].rearrange("n g d -> n (g d)"))
             x2_t = const.tile([P, 4096], BF16, name="x2_sb%d" % q)
             nc.sync.dma_start(out=x2_t[:], in_=x2[rows].rearrange("n g d -> n (g d)"))
             x12_sb.append((x1_t, x2_t))
@@ -72,30 +75,41 @@ def tile_cin_pb_t_kernel(tc, x, x1, x2, h2, w3, b3, out_w, out_b, out):
         )
         xw_words = xw[:].bitcast(F32)
 
-        w_t = ps_z.tile([P, 1024], BF16, name="w_t", tag="z")
-        for h in range(2):
-            for f in range(4):
-                k = h * 4 + f
-                nc.tensor.transpose(w_t[:, k * P:(k + 1) * P], w3_sb[:, h, f * P:(f + 1) * P], ident_b[:])
-        w_g = const.tile([P, 1024], BF16, name="w_g", align_bytes=64)
-        nc.vector.tensor_copy(
-            out=w_g[:].rearrange("p (h o f) -> p h o f", h=2, f=4),
-            in_=w_t[:].rearrange("p (h f o) -> p h o f", h=2, f=4),
-        )
-        ow_g = const.tile([P, 512], BF16, name="ow_g", align_bytes=64)
-        nc.vector.tensor_copy(
-            out=ow_g[:].rearrange("p (j t) -> p j t", t=4),
-            in_=ow_sb[:].rearrange("p t j -> p j t"),
-        )
         w_codes = const.tile([P, 256], U32, name="w_codes", align_bytes=64)
         w_scales = const.tile([P, 256], U8, name="w_scales", align_bytes=64)
-        nc.vector.quantize_mx(out=w_codes[:].bitcast(FP8X4), scales=w_scales[:], in_=w_g[:])
         ow_codes = const.tile([P, 128], U32, name="ow_codes", align_bytes=64)
         ow_scales = const.tile([P, 128], U8, name="ow_scales", align_bytes=64)
-        nc.vector.quantize_mx(out=ow_codes[:].bitcast(FP8X4), scales=ow_scales[:], in_=ow_g[:])
+
+        def prep_w3():
+            w_t = ps_z.tile([P, 1024], BF16, name="w_t", tag="z")
+            for h in range(2):
+                for f in range(4):
+                    k = h * 4 + f
+                    nc.tensor.transpose(w_t[:, k * P:(k + 1) * P], w3_sb[:, h, f * P:(f + 1) * P], ident_b[:])
+            w_g = const.tile([P, 1024], BF16, name="w_g", align_bytes=64)
+            nc.vector.tensor_copy(
+                out=w_g[:].rearrange("p (h o f) -> p h o f", h=2, f=4),
+                in_=w_t[:].rearrange("p (h f o) -> p h o f", h=2, f=4),
+            )
+            nc.vector.quantize_mx(out=w_codes[:].bitcast(FP8X4), scales=w_scales[:], in_=w_g[:])
+
+        def prep_ow():
+            ow_g = const.tile([P, 512], BF16, name="ow_g", align_bytes=64)
+            nc.vector.tensor_copy(
+                out=ow_g[:].rearrange("p (j t) -> p j t", t=4),
+                in_=ow_sb[:].rearrange("p t j -> p j t"),
+            )
+            nc.vector.quantize_mx(out=ow_codes[:].bitcast(FP8X4), scales=ow_scales[:], in_=ow_g[:])
 
         b3_f = const.tile([P, 2], F32, name="b3_f")
         nc.gpsimd.tensor_copy(out=b3_f[:], in_=b3_bf[:])
+        b3_neg = const.tile([P, 2], F32, name="b3_neg")
+        nc.gpsimd.tensor_scalar(out=b3_neg[:], in0=b3_bf[:], scalar1=-1.0, scalar2=0.0, op0=ALU.mult, op1=ALU.add)
+        b3_n = const.tile([P, 2], F32, name="b3_n")
+        nc.gpsimd.tensor_scalar(
+            out=b3_n[:], in0=b3_bf[:], scalar1=float(len(V_CT)), scalar2=0.0, op0=ALU.mult, op1=ALU.add
+        )
+        junk = const.tile([P, 32], BF16, name="junk")
 
         ht = {}
         hd = {}
@@ -105,6 +119,7 @@ def tile_cin_pb_t_kernel(tc, x, x1, x2, h2, w3, b3, out_w, out_b, out):
         zs = {}
         ys = {}
         accs = {}
+        avs = {}
         pls = {}
         st2 = {}
 
@@ -180,39 +195,75 @@ def tile_cin_pb_t_kernel(tc, x, x1, x2, h2, w3, b3, out_w, out_b, out):
                 )
                 zs[(i, h)] = z
 
+        def on_vector(i, h):
+            return h == V_H and (i % 8) in V_CT
+
         def relu_s(i):
             for h in range(2):
-                y = y_pool.tile([P, 512], F32, name="y", tag="y")
-                nc.scalar.activation(out=y[:], in_=zs[(i, h)][:], func=ACT.Relu, bias=b3_f[:, h:h + 1], scale=1.0)
-                ys[(i, h)] = y
+                if not on_vector(i, h):
+                    y = y_pool.tile([P, 512], F32, name="y", tag="y")
+                    nc.scalar.activation(
+                        out=y[:], in_=zs[(i, h)][:], func=ACT.Relu, bias=b3_f[:, h:h + 1], scale=1.0
+                    )
+                    ys[(i, h)] = y
+
+        def relu_v(i):
+            q, c = divmod(i, 8)
+            h = V_H
+            if on_vector(i, h):
+                if c == V_CT[0]:
+                    av = av_pool.tile([P, 512], F32, name="av", tag="av")
+                    avs[q] = av
+                    nc.vector.tensor_scalar(
+                        out=av[:], in0=zs[(i, h)][:], scalar1=b3_neg[:, h:h + 1], scalar2=b3_n[:, h:h + 1],
+                        op0=ALU.max, op1=ALU.add,
+                    )
+                else:
+                    av = avs[q]
+                    nc.vector.scalar_tensor_tensor(
+                        out=av[:], in0=zs[(i, h)][:], scalar=b3_neg[:, h:h + 1], in1=av[:], op0=ALU.max, op1=ALU.add,
+                    )
 
         def acc_t(i):
             q, c = divmod(i, 8)
             if c == 0:
                 accs[q] = ps_acc.tile([P, 256], F32, name="acc", tag="acc")
             acc = accs[q]
-            for h in range(2):
+            todo = [(ys[(i, h)], h) for h in range(2) if not on_vector(i, h)]
+            if c == 7:
+                todo.append((avs[q], V_H))
+            for k, (src, h) in enumerate(todo):
                 for dl in range(4):
                     nc.tensor.matmul(
                         out=acc[:, h * P:(h + 1) * P],
-                        lhsT=ys[(i, h)][:, dl * P:(dl + 1) * P],
+                        lhsT=src[:, dl * P:(dl + 1) * P],
                         rhs=ident_f[:],
-                        start=(c == 0 and h == 0 and dl == 0),
-                        stop=(c == 7 and h == 1 and dl == 3),
+                        start=(c == 0 and k == 0 and dl == 0),
+                        stop=(c == 7 and k == len(todo) - 1 and dl == 3),
                         is_transpose=True,
                     )
 
         def pool12(i):
-            q, r = divmod(i, 8)
-            t, part = divmod(r, 4)
-            if r == 0:
+            q, c = divmod(i, 8)
+            if c == 0:
                 pls[q] = s2_pool.tile([P, 512], BF16, name="pl", tag="pl")
-            src = x12_sb[q][t][:].rearrange("p (c d) -> p c d", d=32)
+            if c in V_POOL:
+                t, lo, hi = V_POOL[c]
+                src = x12_sb[q][t][:].rearrange("p (c d) -> p c d", d=32)
+                with nc.allow_low_precision(reason="float32 sum, rounded once to bfloat16 for quantize_mx"):
+                    nc.vector.tensor_reduce(
+                        out=pls[q][:, t * P + lo:t * P + hi], in_=src[:, lo:hi, :], axis=AX.X, op=ALU.add
+                    )
+
+        def pool_s(i):
+            q, c = divmod(i, 8)
+            first = 32 + sum(S_POOL[:c])
             with nc.allow_low_precision(reason="float32 sum, rounded once to bfloat16 for quantize_mx"):
-                nc.vector.tensor_reduce(
-                    out=pls[q][:, t * P + part * 32:t * P + (part + 1) * 32],
-                    in_=src[:, part * 32:(part + 1) * 32, :], axis=AX.X, op=ALU.add,
-                )
+                for ch in range(first, first + S_POOL[c]):
+                    nc.scalar.activation(
+                        out=junk[:], in_=x12_sb[q][1][:, ch * 32:(ch + 1) * 32], func=ACT.Copy,
+                        accum_out=pls[q][:, P + ch:P + ch + 1],
+                    )
 
         def acc_exit(q):
             nc.scalar.copy(out=pls[q][:, 256:512], in_=accs[q][:])
@@ -253,16 +304,21 @@ def tile_cin_pb_t_kernel(tc, x, x1, x2, h2, w3, b3, out_w, out_b, out):
 
         t_xb(0)
         t_xb(1)
-        for i in range(-5, NCT + 5):
+        t_h(0)
+        prep_w3()
+        for i in range(-3, NCT + 5):
             q9, r9 = divmod(i - 9, 8)
             q10, r10 = divmod(i - 10, 8)
             q11, r11 = divmod(i - 11, 8)
             if i % 2 == 0 and 0 <= i // 2 + 1 < 16:
                 hd_exit(i // 2 + 1, 1)
+            if 0 <= i - 1 < NCT:
+                relu_s(i - 1)
+                relu_v(i - 1)
             if r9 == 0 and 0 <= q9 < NQ:
                 acc_exit(q9)
             if 0 <= i - 1 < NCT:
-                relu_s(i - 1)
+                pool_s(i - 1)
             if 0 <= i < NCT:
                 quant(i)
             if r10 == 0 and 0 <= q10 < NQ:
@@ -279,8 +335,10 @@ def tile_cin_pb_t_kernel(tc, x, x1, x2, h2, w3, b3, out_w, out_b, out):
                 acc_t(i - 1)
             if 0 <= i + 1 < NCT:
                 mult(i + 1)
-            if 0 <= i + 5 < NCT:
-                pool12(i + 5)
+            if 0 <= i < NCT:
+                pool12(i)
+            if i == 3:
+                prep_ow()
             if r10 == 0 and 0 <= q10 < NQ:
                 s2_quant(q10)
             if i % 2 != 0 and 0 <= (i - 1) // 2 + 2 < 16:

@@ -17,10 +17,6 @@ AX = mybir.AxisListType
 P = 128
 NQ = 4
 NCT = 32
-V_CT = (1, 3, 5, 7)
-V_H = 1
-V_POOL = {0: (0, 0, 32), 2: (0, 32, 64), 4: (0, 64, 96), 6: (0, 96, 128), 1: (1, 0, 16), 5: (1, 16, 32)}
-S_POOL = (8, 16, 8, 16, 8, 16, 8, 16)
 
 
 def tile_cin_pb_t_kernel(tc, x, x1, x2, h2, w3, b3, out_w, out_b, out):
@@ -30,7 +26,6 @@ def tile_cin_pb_t_kernel(tc, x, x1, x2, h2, w3, b3, out_w, out_b, out):
         hd_pool = ctx.enter_context(tc.tile_pool(name="hdp", bufs=3))
         p_pool = ctx.enter_context(tc.tile_pool(name="pp", bufs=3))
         y_pool = ctx.enter_context(tc.tile_pool(name="yp", bufs=4))
-        av_pool = ctx.enter_context(tc.tile_pool(name="avp", bufs=2))
         s2_pool = ctx.enter_context(tc.tile_pool(name="s2p", bufs=2))
         ps_xb = ctx.enter_context(tc.psum_pool(name="psxb", bufs=4))
         ps_z = ctx.enter_context(tc.psum_pool(name="psz", bufs=2))
@@ -103,13 +98,6 @@ def tile_cin_pb_t_kernel(tc, x, x1, x2, h2, w3, b3, out_w, out_b, out):
 
         b3_f = const.tile([P, 2], F32, name="b3_f")
         nc.gpsimd.tensor_copy(out=b3_f[:], in_=b3_bf[:])
-        b3_neg = const.tile([P, 2], F32, name="b3_neg")
-        nc.gpsimd.tensor_scalar(out=b3_neg[:], in0=b3_bf[:], scalar1=-1.0, scalar2=0.0, op0=ALU.mult, op1=ALU.add)
-        b3_n = const.tile([P, 2], F32, name="b3_n")
-        nc.gpsimd.tensor_scalar(
-            out=b3_n[:], in0=b3_bf[:], scalar1=float(len(V_CT)), scalar2=0.0, op0=ALU.mult, op1=ALU.add
-        )
-        junk = const.tile([P, 32], BF16, name="junk")
 
         ht = {}
         hd = {}
@@ -119,7 +107,6 @@ def tile_cin_pb_t_kernel(tc, x, x1, x2, h2, w3, b3, out_w, out_b, out):
         zs = {}
         ys = {}
         accs = {}
-        avs = {}
         pls = {}
         st2 = {}
 
@@ -195,75 +182,46 @@ def tile_cin_pb_t_kernel(tc, x, x1, x2, h2, w3, b3, out_w, out_b, out):
                 )
                 zs[(i, h)] = z
 
-        def on_vector(i, h):
-            return h == V_H and (i % 8) in V_CT
-
         def relu_s(i):
             for h in range(2):
-                if not on_vector(i, h):
-                    y = y_pool.tile([P, 512], F32, name="y", tag="y")
+                y = y_pool.tile([P, 512], F32, name="y", tag="y")
+                if i == NCT - 1 and h == 1:
+                    nc.vector.tensor_scalar(
+                        out=y[:], in0=zs[(i, h)][:], scalar1=b3_f[:, h:h + 1], scalar2=0.0, op0=ALU.add, op1=ALU.max
+                    )
+                else:
                     nc.scalar.activation(
                         out=y[:], in_=zs[(i, h)][:], func=ACT.Relu, bias=b3_f[:, h:h + 1], scale=1.0
                     )
-                    ys[(i, h)] = y
-
-        def relu_v(i):
-            q, c = divmod(i, 8)
-            h = V_H
-            if on_vector(i, h):
-                if c == V_CT[0]:
-                    av = av_pool.tile([P, 512], F32, name="av", tag="av")
-                    avs[q] = av
-                    nc.vector.tensor_scalar(
-                        out=av[:], in0=zs[(i, h)][:], scalar1=b3_neg[:, h:h + 1], scalar2=b3_n[:, h:h + 1],
-                        op0=ALU.max, op1=ALU.add,
-                    )
-                else:
-                    av = avs[q]
-                    nc.vector.scalar_tensor_tensor(
-                        out=av[:], in0=zs[(i, h)][:], scalar=b3_neg[:, h:h + 1], in1=av[:], op0=ALU.max, op1=ALU.add,
-                    )
+                ys[(i, h)] = y
 
         def acc_t(i):
             q, c = divmod(i, 8)
             if c == 0:
                 accs[q] = ps_acc.tile([P, 256], F32, name="acc", tag="acc")
             acc = accs[q]
-            todo = [(ys[(i, h)], h) for h in range(2) if not on_vector(i, h)]
-            if c == 7:
-                todo.append((avs[q], V_H))
-            for k, (src, h) in enumerate(todo):
+            for h in range(2):
                 for dl in range(4):
                     nc.tensor.matmul(
                         out=acc[:, h * P:(h + 1) * P],
-                        lhsT=src[:, dl * P:(dl + 1) * P],
+                        lhsT=ys[(i, h)][:, dl * P:(dl + 1) * P],
                         rhs=ident_f[:],
-                        start=(c == 0 and k == 0 and dl == 0),
-                        stop=(c == 7 and k == len(todo) - 1 and dl == 3),
+                        start=(c == 0 and h == 0 and dl == 0),
+                        stop=(c == 7 and h == 1 and dl == 3),
                         is_transpose=True,
                     )
 
         def pool12(i):
-            q, c = divmod(i, 8)
-            if c == 0:
+            q, r = divmod(i, 8)
+            t, part = divmod(r, 4)
+            if r == 0:
                 pls[q] = s2_pool.tile([P, 512], BF16, name="pl", tag="pl")
-            if c in V_POOL:
-                t, lo, hi = V_POOL[c]
-                src = x12_sb[q][t][:].rearrange("p (c d) -> p c d", d=32)
-                with nc.allow_low_precision(reason="float32 sum, rounded once to bfloat16 for quantize_mx"):
-                    nc.vector.tensor_reduce(
-                        out=pls[q][:, t * P + lo:t * P + hi], in_=src[:, lo:hi, :], axis=AX.X, op=ALU.add
-                    )
-
-        def pool_s(i):
-            q, c = divmod(i, 8)
-            first = 32 + sum(S_POOL[:c])
+            src = x12_sb[q][t][:].rearrange("p (c d) -> p c d", d=32)
             with nc.allow_low_precision(reason="float32 sum, rounded once to bfloat16 for quantize_mx"):
-                for ch in range(first, first + S_POOL[c]):
-                    nc.scalar.activation(
-                        out=junk[:], in_=x12_sb[q][1][:, ch * 32:(ch + 1) * 32], func=ACT.Copy,
-                        accum_out=pls[q][:, P + ch:P + ch + 1],
-                    )
+                nc.vector.tensor_reduce(
+                    out=pls[q][:, t * P + part * 32:t * P + (part + 1) * 32],
+                    in_=src[:, part * 32:(part + 1) * 32, :], axis=AX.X, op=ALU.add,
+                )
 
         def acc_exit(q):
             nc.scalar.copy(out=pls[q][:, 256:512], in_=accs[q][:])
@@ -314,11 +272,8 @@ def tile_cin_pb_t_kernel(tc, x, x1, x2, h2, w3, b3, out_w, out_b, out):
                 hd_exit(i // 2 + 1, 1)
             if 0 <= i - 1 < NCT:
                 relu_s(i - 1)
-                relu_v(i - 1)
             if r9 == 0 and 0 <= q9 < NQ:
                 acc_exit(q9)
-            if 0 <= i - 1 < NCT:
-                pool_s(i - 1)
             if 0 <= i < NCT:
                 quant(i)
             if r10 == 0 and 0 <= q10 < NQ:

@@ -17,6 +17,7 @@ AX = mybir.AxisListType
 P = 128
 NQ = 4
 NCT = 32
+POOL_ROUND = tuple(range(NCT - 3)) + (NCT - 1, NCT, NCT)
 
 
 def tile_cin_pb_t_kernel(tc, x, x1, x2, h2, w3, b3, out_w, out_b, out):
@@ -268,8 +269,6 @@ def tile_cin_pb_t_kernel(tc, x, x1, x2, h2, w3, b3, out_w, out_b, out):
             q9, r9 = divmod(i - 9, 8)
             q10, r10 = divmod(i - 10, 8)
             q11, r11 = divmod(i - 11, 8)
-            if i % 2 == 0 and 0 <= i // 2 + 1 < 16:
-                hd_exit(i // 2 + 1, 1)
             if 0 <= i - 1 < NCT:
                 relu_s(i - 1)
             if r9 == 0 and 0 <= q9 < NQ:
@@ -290,12 +289,15 @@ def tile_cin_pb_t_kernel(tc, x, x1, x2, h2, w3, b3, out_w, out_b, out):
                 acc_t(i - 1)
             if 0 <= i + 1 < NCT:
                 mult(i + 1)
-            if 0 <= i < NCT:
-                pool12(i)
+            for k in range(NCT):
+                if POOL_ROUND[k] == i:
+                    pool12(k)
             if i == 3:
                 prep_ow()
             if r10 == 0 and 0 <= q10 < NQ:
                 s2_quant(q10)
+            if i % 2 == 0 and 0 <= i // 2 + 1 < 16:
+                hd_exit(i // 2 + 1, 1)
             if i % 2 != 0 and 0 <= (i - 1) // 2 + 2 < 16:
                 hd_exit((i - 1) // 2 + 2, 0)
             if i % 2 == 0 and 0 <= i // 2 + 2 < 16:

@@ -17,7 +17,8 @@ AX = mybir.AxisListType
 P = 128
 NQ = 4
 NCT = 32
-POOL_ROUND = tuple(range(NCT - 3)) + (NCT - 1, NCT, NCT)
+POOL_ROUND = (-3,) * 4 + tuple(r for r in range(NCT - 3) if r % 7 != 6) + (NCT - 1, NCT, NCT)
+assert len(POOL_ROUND) == NCT
 
 
 def tile_cin_pb_t_kernel(tc, x, x1, x2, h2, w3, b3, out_w, out_b, out):
@@ -37,6 +38,7 @@ def tile_cin_pb_t_kernel(tc, x, x1, x2, h2, w3, b3, out_w, out_b, out):
         x_sb = const.tile([P, NQ, 128], BF16, name="x_sb")
         nc.sync.dma_start(out=x_sb[:], in_=x.rearrange("(q p) f d -> p q (f d)", p=P))
         w3_sb = const.tile([P, 2, 512], BF16, name="w3_sb")
+        nc.sync.dma_start(out=w3_sb[:], in_=w3.rearrange("(h p) f g -> p h (f g)", p=P))
         b3_bf = const.tile([P, 2], BF16, name="b3_bf")
         with nc.allow_non_contiguous_dma(reason="256 bias values, one per partition and half"):
             nc.scalar.dma_start(out=b3_bf[:], in_=b3.rearrange("(h p) -> p h", p=P))
@@ -50,11 +52,12 @@ def tile_cin_pb_t_kernel(tc, x, x1, x2, h2, w3, b3, out_w, out_b, out):
             rows = slice(q * P, (q + 1) * P)
             h2_t = const.tile([P, 4096], BF16, name="h2_sb%d" % q)
             x1_t = const.tile([P, 4096], BF16, name="x1_sb%d" % q)
+            if q == 0:
+                nc.sync.dma_start(out=x1_t[:], in_=x1[rows].rearrange("n g d -> n (g d)"))
             nc.sync.dma_start(out=h2_t[:], in_=h2[rows].rearrange("n g d -> n (g d)"))
             h2_sb.append(h2_t)
-            if q == 0:
-                nc.sync.dma_start(out=w3_sb[:], in_=w3.rearrange("(h p) f g -> p h (f g)", p=P))
-            nc.sync.dma_start(out=x1_t[:], in_=x1[rows].rearrange("n g d -> n (g d)"))
+            if q != 0:
+                nc.sync.dma_start(out=x1_t[:], in_=x1[rows].rearrange("n g d -> n (g d)"))
             x2_t = const.tile([P, 4096], BF16, name="x2_sb%d" % q)
             nc.sync.dma_start(out=x2_t[:], in_=x2[rows].rearrange("n g d -> n (g d)"))
             x12_sb.append((x1_t, x2_t))
@@ -261,10 +264,11 @@ def tile_cin_pb_t_kernel(tc, x, x1, x2, h2, w3, b3, out_w, out_b, out):
             nc.vector.tensor_tensor(out=res[:], in0=st2[(q, "o2")][:], in1=outb[:], op=ALU.add)
             nc.sync.dma_start(out=out[q * P:(q + 1) * P, :], in_=res[:])
 
+        prep_ow()
+        prep_w3()
         t_xb(0)
         t_xb(1)
         t_h(0)
-        prep_w3()
         for i in range(-3, NCT + 5):
             q9, r9 = divmod(i - 9, 8)
             q10, r10 = divmod(i - 10, 8)
@@ -292,8 +296,6 @@ def tile_cin_pb_t_kernel(tc, x, x1, x2, h2, w3, b3, out_w, out_b, out):
             for k in range(NCT):
                 if POOL_ROUND[k] == i:
                     pool12(k)
-            if i == 3:
-                prep_ow()
             if r10 == 0 and 0 <= q10 < NQ:
                 s2_quant(q10)
             if i % 2 == 0 and 0 <= i // 2 + 1 < 16:

@@ -17,8 +17,10 @@ AX = mybir.AxisListType
 P = 128
 NQ = 4
 NCT = 32
-POOL_ROUND = (-3,) * 4 + tuple(r for r in range(NCT - 3) if r % 7 != 6) + (NCT - 1, NCT, NCT)
-assert len(POOL_ROUND) == NCT
+NPE = 104
+CHUNK = 19
+NCHUNK = (256 - NPE) // CHUNK
+POOL_ROUND = [(1 + 7 * q + part, q, part) for q in range(NQ) for part in range(NCHUNK)]
 
 
 def tile_cin_pb_t_kernel(tc, x, x1, x2, h2, w3, b3, out_w, out_b, out):
@@ -51,16 +53,12 @@ def tile_cin_pb_t_kernel(tc, x, x1, x2, h2, w3, b3, out_w, out_b, out):
         for q in range(NQ):
             rows = slice(q * P, (q + 1) * P)
             h2_t = const.tile([P, 4096], BF16, name="h2_sb%d" % q)
-            x1_t = const.tile([P, 4096], BF16, name="x1_sb%d" % q)
-            if q == 0:
-                nc.sync.dma_start(out=x1_t[:], in_=x1[rows].rearrange("n g d -> n (g d)"))
             nc.sync.dma_start(out=h2_t[:], in_=h2[rows].rearrange("n g d -> n (g d)"))
             h2_sb.append(h2_t)
-            if q != 0:
-                nc.sync.dma_start(out=x1_t[:], in_=x1[rows].rearrange("n g d -> n (g d)"))
-            x2_t = const.tile([P, 4096], BF16, name="x2_sb%d" % q)
-            nc.sync.dma_start(out=x2_t[:], in_=x2[rows].rearrange("n g d -> n (g d)"))
-            x12_sb.append((x1_t, x2_t))
+            x12_t = const.tile([P, 8192], BF16, name="x12_sb%d" % q)
+            nc.sync.dma_start(out=x12_t[:, 0:4096], in_=x1[rows].rearrange("n g d -> n (g d)"))
+            nc.sync.dma_start(out=x12_t[:, 4096:8192], in_=x2[rows].rearrange("n g d -> n (g d)"))
+            x12_sb.append(x12_t)
 
         ident_f = const.tile([P, P], F32, name="ident_f")
         make_identity(nc, ident_f[:])
@@ -199,10 +197,19 @@ def tile_cin_pb_t_kernel(tc, x, x1, x2, h2, w3, b3, out_w, out_b, out):
                     )
                 ys[(i, h)] = y
 
-        def acc_t(i):
+        def acc_x(i):
             q, c = divmod(i, 8)
             if c == 0:
-                accs[q] = ps_acc.tile([P, 256], F32, name="acc", tag="acc")
+                accs[q] = ps_acc.tile([P, 256 + NPE], F32, name="acc", tag="acc")
+            xv = x12_sb[q][:].rearrange("p (c d) -> p c d", d=32)
+            for dl in range(4):
+                nc.tensor.matmul(
+                    out=accs[q][:, 256:256 + NPE], lhsT=ident_b[:], rhs=xv[:, 0:NPE, 4 * c + dl],
+                    start=(c == 0 and dl == 0), stop=False,
+                )
+
+        def acc_t(i):
+            q, c = divmod(i, 8)
             acc = accs[q]
             for h in range(2):
                 for dl in range(4):
@@ -210,25 +217,22 @@ def tile_cin_pb_t_kernel(tc, x, x1, x2, h2, w3, b3, out_w, out_b, out):
                         out=acc[:, h * P:(h + 1) * P],
                         lhsT=ys[(i, h)][:, dl * P:(dl + 1) * P],
                         rhs=ident_f[:],
-                        start=(c == 0 and h == 0 and dl == 0),
+                        start=False,
                         stop=(c == 7 and h == 1 and dl == 3),
                         is_transpose=True,
                     )
 
-        def pool12(i):
-            q, r = divmod(i, 8)
-            t, part = divmod(r, 4)
-            if r == 0:
+        def pool12(q, part):
+            if part == 0:
                 pls[q] = s2_pool.tile([P, 512], BF16, name="pl", tag="pl")
-            src = x12_sb[q][t][:].rearrange("p (c d) -> p c d", d=32)
+            src = x12_sb[q][:].rearrange("p (c d) -> p c d", d=32)
+            chans = slice(NPE + part * CHUNK, NPE + (part + 1) * CHUNK)
             with nc.allow_low_precision(reason="float32 sum, rounded once to bfloat16 for quantize_mx"):
-                nc.vector.tensor_reduce(
-                    out=pls[q][:, t * P + part * 32:t * P + (part + 1) * 32],
-                    in_=src[:, part * 32:(part + 1) * 32, :], axis=AX.X, op=ALU.add,
-                )
+                nc.vector.tensor_reduce(out=pls[q][:, chans], in_=src[:, chans, :], axis=AX.X, op=ALU.add)
 
         def acc_exit(q):
-            nc.scalar.copy(out=pls[q][:, 256:512], in_=accs[q][:])
+            nc.scalar.copy(out=pls[q][:, 256:512], in_=accs[q][:, 0:256])
+            nc.scalar.copy(out=pls[q][:, 0:NPE], in_=accs[q][:, 256:256 + NPE])
 
         def s2_transpose(q):
             pt2 = ps_z.tile([P, 512], BF16, name="pt2", tag="z")
@@ -290,12 +294,13 @@ def tile_cin_pb_t_kernel(tc, x, x1, x2, h2, w3, b3, out_w, out_b, out):
             if 0 <= i < NCT:
                 mx(i)
             if 0 <= i - 1 < NCT:
+                acc_x(i - 1)
                 acc_t(i - 1)
             if 0 <= i + 1 < NCT:
                 mult(i + 1)
-            for k in range(NCT):
-                if POOL_ROUND[k] == i:
-                    pool12(k)
+            for r, q, part in POOL_ROUND:
+                if r == i:
+                    pool12(q, part)
             if r10 == 0 and 0 <= q10 < NQ:
                 s2_quant(q10)
             if i % 2 == 0 and 0 <= i // 2 + 1 < 16:

@@ -29,6 +29,7 @@ def tile_cin_pb_t_kernel(tc, x, x1, x2, h2, w3, b3, out_w, out_b, out):
         const = ctx.enter_context(tc.tile_pool(name="const", bufs=1))
         hd_pool = ctx.enter_context(tc.tile_pool(name="hdp", bufs=3))
         p_pool = ctx.enter_context(tc.tile_pool(name="pp", bufs=3))
+        xb_pool = ctx.enter_context(tc.tile_pool(name="xbp", bufs=2))
         y_pool = ctx.enter_context(tc.tile_pool(name="yp", bufs=4))
         s2_pool = ctx.enter_context(tc.tile_pool(name="s2p", bufs=2))
         ps_xb = ctx.enter_context(tc.psum_pool(name="psxb", bufs=4))
@@ -50,15 +51,20 @@ def tile_cin_pb_t_kernel(tc, x, x1, x2, h2, w3, b3, out_w, out_b, out):
         nc.scalar.dma_start(out=outb[:], in_=out_b.partition_broadcast(P))
         h2_sb = []
         x12_sb = []
-        for q in range(NQ):
+
+        def load_q(q):
             rows = slice(q * P, (q + 1) * P)
             h2_t = const.tile([P, 4096], BF16, name="h2_sb%d" % q)
             nc.sync.dma_start(out=h2_t[:], in_=h2[rows].rearrange("n g d -> n (g d)"))
             h2_sb.append(h2_t)
+            if q == 1 or q == 2:
+                load_xb(q)
             x12_t = const.tile([P, 8192], BF16, name="x12_sb%d" % q)
             nc.sync.dma_start(out=x12_t[:, 0:4096], in_=x1[rows].rearrange("n g d -> n (g d)"))
             nc.sync.dma_start(out=x12_t[:, 4096:8192], in_=x2[rows].rearrange("n g d -> n (g d)"))
             x12_sb.append(x12_t)
+
+        load_q(0)
 
         ident_f = const.tile([P, P], F32, name="ident_f")
         make_identity(nc, ident_f[:])
@@ -71,6 +77,23 @@ def tile_cin_pb_t_kernel(tc, x, x1, x2, h2, w3, b3, out_w, out_b, out):
             in_=x_sb[:].rearrange("p q (f d) -> p q d f", f=4),
         )
         xw_words = xw[:].bitcast(F32)
+
+        def x_rows(q):
+            return out[320 + 64 * (q - 1):320 + 64 * q, :].rearrange("r w -> (r w)")
+
+        for q in range(1, NQ):
+            nc.sync.dma_start(
+                out=x_rows(q).rearrange("(n w) -> n w", w=64), in_=xw_words[:, 64 * q:64 * (q + 1)]
+            )
+        xbs_q = {}
+
+        def load_xb(q):
+            xb_t = xb_pool.tile([P, 8192], F32, name="xb_t", tag="xbq")
+            nc.sync.dma_start(out=xb_t[:], in_=x_rows(q).partition_broadcast(P))
+            xbs_q[q] = xb_t
+
+        for q in range(1, NQ):
+            load_q(q)
 
         w_codes = const.tile([P, 256], U32, name="w_codes", align_bytes=64)
         w_scales = const.tile([P, 256], U8, name="w_scales", align_bytes=64)
@@ -152,6 +175,18 @@ def tile_cin_pb_t_kernel(tc, x, x1, x2, h2, w3, b3, out_w, out_b, out):
         def mult(i):
             u = i // 2
             pt = p_pool.tile([P, 2048], BF16, name="pt", tag="pt", align_bytes=64)
+            q, c = divmod(i, 8)
+            if q > 0:
+                d0 = (i % 2) * 4
+                xv = xbs_q[q][:].bitcast(BF16).rearrange("p (n d fp e) -> p d n fp e", d=32, fp=2, e=2)
+                nc.vector.tensor_tensor(
+                    out=pt[:].rearrange("p (d n fp e) -> p d n fp e", d=4, fp=2, e=2),
+                    in0=hd[u][:, d0:d0 + 4, :, :].unsqueeze(3).to_broadcast([P, 4, 128, 2, 2]),
+                    in1=xv[:, 4 * c:4 * c + 4],
+                    op=ALU.mult,
+                )
+                pts[i] = pt
+                return
             for s in range(2):
                 dloc = (i % 2) * 4 + 2 * s
                 in0 = hd[u][:, dloc:dloc + 2, :, :].rearrange("p d n u -> p (d n) u")
@@ -286,7 +321,9 @@ def tile_cin_pb_t_kernel(tc, x, x1, x2, h2, w3, b3, out_w, out_b, out):
             if r10 == 0 and 0 <= q10 < NQ:
                 s2_transpose(q10)
                 s2_group(q10)
-            if 2 <= i + 2 < NCT:
+            if i == 16:
+                load_xb(3)
+            if 2 <= i + 2 < 8:
                 t_xb(i + 2)
             if r11 == 0 and 0 <= q11 < NQ:
                 s2_mx(q11)

@@ -18,9 +18,12 @@ P = 128
 NQ = 4
 NCT = 32
 NPE = 104
-CHUNK = 19
+CHUNK = 38
 NCHUNK = (256 - NPE) // CHUNK
-POOL_ROUND = [(1 + 7 * q + part, q, part) for q in range(NQ) for part in range(NCHUNK)]
+POOL_ROUND = [(2 + (NCHUNK * q + part) * 27 // 16, q, part) for q in range(NQ) for part in range(NCHUNK)]
+PE_POOL_ROUND = [(9 + k * 22 // 32, k // 8, k % 8) for k in range(8 * NQ)]
+PE_EXIT_ROUND = {q: 1 + PE_POOL_ROUND[8 * q + 7][0] for q in range(NQ)}
+S2_ROUND = {q: max(8 * q + 10, PE_EXIT_ROUND[q] + 2) for q in range(NQ)}
 
 
 def tile_cin_pb_t_kernel(tc, x, x1, x2, h2, w3, b3, out_w, out_b, out):
@@ -31,6 +34,7 @@ def tile_cin_pb_t_kernel(tc, x, x1, x2, h2, w3, b3, out_w, out_b, out):
         p_pool = ctx.enter_context(tc.tile_pool(name="pp", bufs=3))
         xb_pool = ctx.enter_context(tc.tile_pool(name="xbp", bufs=2))
         y_pool = ctx.enter_context(tc.tile_pool(name="yp", bufs=4))
+        pl_pool = ctx.enter_context(tc.tile_pool(name="plp", bufs=4))
         s2_pool = ctx.enter_context(tc.tile_pool(name="s2p", bufs=2))
         ps_xb = ctx.enter_context(tc.psum_pool(name="psxb", bufs=4))
         ps_z = ctx.enter_context(tc.psum_pool(name="psz", bufs=2))
@@ -57,8 +61,9 @@ def tile_cin_pb_t_kernel(tc, x, x1, x2, h2, w3, b3, out_w, out_b, out):
             h2_t = const.tile([P, 4096], BF16, name="h2_sb%d" % q)
             nc.sync.dma_start(out=h2_t[:], in_=h2[rows].rearrange("n g d -> n (g d)"))
             h2_sb.append(h2_t)
-            if q == 1 or q == 2:
-                load_xb(q)
+
+        def load_x12(q):
+            rows = slice(q * P, (q + 1) * P)
             x12_t = const.tile([P, 8192], BF16, name="x12_sb%d" % q)
             nc.sync.dma_start(out=x12_t[:, 0:4096], in_=x1[rows].rearrange("n g d -> n (g d)"))
             nc.sync.dma_start(out=x12_t[:, 4096:8192], in_=x2[rows].rearrange("n g d -> n (g d)"))
@@ -92,8 +97,12 @@ def tile_cin_pb_t_kernel(tc, x, x1, x2, h2, w3, b3, out_w, out_b, out):
             nc.sync.dma_start(out=xb_t[:], in_=x_rows(q).partition_broadcast(P))
             xbs_q[q] = xb_t
 
+        load_x12(0)
         for q in range(1, NQ):
             load_q(q)
+            if q < 3:
+                load_xb(q)
+            load_x12(q)
 
         w_codes = const.tile([P, 256], U32, name="w_codes", align_bytes=64)
         w_scales = const.tile([P, 256], U8, name="w_scales", align_bytes=64)
@@ -133,6 +142,7 @@ def tile_cin_pb_t_kernel(tc, x, x1, x2, h2, w3, b3, out_w, out_b, out):
         ys = {}
         accs = {}
         pls = {}
+        xps = {}
         st2 = {}
 
         def t_h(u):
@@ -207,7 +217,10 @@ def tile_cin_pb_t_kernel(tc, x, x1, x2, h2, w3, b3, out_w, out_b, out):
         def mx(i):
             codes, scales = cds[i]
             for h in range(2):
-                z = ps_z.tile([P, 512], F32, name="z", tag="z")
+                if i < 8:
+                    z = ps_z.tile([P, 512], F32, name="z", tag="z")
+                else:
+                    z = ps_xb.tile([P, 512], F32, name="z", tag="xb")
                 nc.tensor.matmul_mx(
                     out=z[:],
                     lhsT=w_codes[:, h * P:(h + 1) * P].bitcast(FP8X4),
@@ -232,19 +245,25 @@ def tile_cin_pb_t_kernel(tc, x, x1, x2, h2, w3, b3, out_w, out_b, out):
                     )
                 ys[(i, h)] = y
 
-        def acc_x(i):
-            q, c = divmod(i, 8)
-            if c == 0:
-                accs[q] = ps_acc.tile([P, 256 + NPE], F32, name="acc", tag="acc")
-            xv = x12_sb[q][:].rearrange("p (c d) -> p c d", d=32)
-            for dl in range(4):
-                nc.tensor.matmul(
-                    out=accs[q][:, 256:256 + NPE], lhsT=ident_b[:], rhs=xv[:, 0:NPE, 4 * c + dl],
-                    start=(c == 0 and dl == 0), stop=False,
+        def pe_pool(q, dg):
+            if dg == 0:
+                xps[q] = ps_z.tile([P, 4 * NPE], F32, name="xp", tag="z")
+            xv = x12_sb[q][:].rearrange("p (c dg dr) -> p c dg dr", dg=8, dr=4)
+            nc.tensor.matmul(
+                out=xps[q][:], lhsT=ident_b[:], rhs=xv[:, 0:NPE, dg, :], start=(dg == 0), stop=(dg == 7)
+            )
+
+        def pe_pool_exit(q):
+            with nc.allow_low_precision(reason="float32 sum, rounded once to bfloat16 for quantize_mx"):
+                nc.vector.tensor_reduce(
+                    out=pls[q][:, 0:NPE], in_=xps[q][:].rearrange("p (c dr) -> p c dr", dr=4),
+                    axis=AX.X, op=ALU.add,
                 )
 
         def acc_t(i):
             q, c = divmod(i, 8)
+            if c == 0:
+                accs[q] = ps_acc.tile([P, 256], F32, name="acc", tag="acc")
             acc = accs[q]
             for h in range(2):
                 for dl in range(4):
@@ -252,14 +271,14 @@ def tile_cin_pb_t_kernel(tc, x, x1, x2, h2, w3, b3, out_w, out_b, out):
                         out=acc[:, h * P:(h + 1) * P],
                         lhsT=ys[(i, h)][:, dl * P:(dl + 1) * P],
                         rhs=ident_f[:],
-                        start=False,
+                        start=(c == 0 and h == 0 and dl == 0),
                         stop=(c == 7 and h == 1 and dl == 3),
                         is_transpose=True,
                     )
 
         def pool12(q, part):
             if part == 0:
-                pls[q] = s2_pool.tile([P, 512], BF16, name="pl", tag="pl")
+                pls[q] = pl_pool.tile([P, 512], BF16, name="pl", tag="pl")
             src = x12_sb[q][:].rearrange("p (c d) -> p c d", d=32)
             chans = slice(NPE + part * CHUNK, NPE + (part + 1) * CHUNK)
             with nc.allow_low_precision(reason="float32 sum, rounded once to bfloat16 for quantize_mx"):
@@ -267,10 +286,9 @@ def tile_cin_pb_t_kernel(tc, x, x1, x2, h2, w3, b3, out_w, out_b, out):
 
         def acc_exit(q):
             nc.scalar.copy(out=pls[q][:, 256:512], in_=accs[q][:, 0:256])
-            nc.scalar.copy(out=pls[q][:, 0:NPE], in_=accs[q][:, 256:256 + NPE])
 
         def s2_transpose(q):
-            pt2 = ps_z.tile([P, 512], BF16, name="pt2", tag="z")
+            pt2 = ps_xb.tile([P, 512], BF16, name="pt2", tag="xb")
             for t in range(4):
                 nc.tensor.transpose(pt2[:, t * P:(t + 1) * P], pls[q][:, t * P:(t + 1) * P], ident_b[:])
             st2[(q, "pt2")] = pt2
@@ -291,7 +309,7 @@ def tile_cin_pb_t_kernel(tc, x, x1, x2, h2, w3, b3, out_w, out_b, out):
 
         def s2_mx(q):
             c2, sc2 = st2[(q, "c2")]
-            o2 = ps_z.tile([P, 128], F32, name="o2", tag="z")
+            o2 = ps_xb.tile([P, 128], F32, name="o2", tag="xb")
             nc.tensor.matmul_mx(
                 out=o2[:], lhsT=c2[:].bitcast(FP8X4), lhsT_scale=sc2[:],
                 rhs=ow_codes[:].bitcast(FP8X4), rhs_scale=ow_scales[:], start=True, stop=True,
@@ -310,36 +328,41 @@ def tile_cin_pb_t_kernel(tc, x, x1, x2, h2, w3, b3, out_w, out_b, out):
         t_h(0)
         for i in range(-3, NCT + 5):
             q9, r9 = divmod(i - 9, 8)
-            q10, r10 = divmod(i - 10, 8)
-            q11, r11 = divmod(i - 11, 8)
             if 0 <= i - 1 < NCT:
                 relu_s(i - 1)
             if r9 == 0 and 0 <= q9 < NQ:
                 acc_exit(q9)
             if 0 <= i < NCT:
                 quant(i)
-            if r10 == 0 and 0 <= q10 < NQ:
-                s2_transpose(q10)
-                s2_group(q10)
+            for q in range(NQ):
+                if i == S2_ROUND[q]:
+                    s2_transpose(q)
+                    s2_group(q)
             if i == 16:
                 load_xb(3)
             if 2 <= i + 2 < 8:
                 t_xb(i + 2)
-            if r11 == 0 and 0 <= q11 < NQ:
-                s2_mx(q11)
-                s2_out(q11)
+            for q in range(NQ):
+                if i == S2_ROUND[q] + 1:
+                    s2_mx(q)
+                    s2_out(q)
             if 0 <= i < NCT:
                 mx(i)
+            for r, q, dg in PE_POOL_ROUND:
+                if r == i:
+                    pe_pool(q, dg)
             if 0 <= i - 1 < NCT:
-                acc_x(i - 1)
                 acc_t(i - 1)
             if 0 <= i + 1 < NCT:
                 mult(i + 1)
             for r, q, part in POOL_ROUND:
                 if r == i:
                     pool12(q, part)
-            if r10 == 0 and 0 <= q10 < NQ:
-                s2_quant(q10)
+            for q in range(NQ):
+                if i == PE_EXIT_ROUND[q]:
+                    pe_pool_exit(q)
+                if i == S2_ROUND[q]:
+                    s2_quant(q)
             if i % 2 == 0 and 0 <= i // 2 + 1 < 16:
                 hd_exit(i // 2 + 1, 1)
             if i % 2 != 0 and 0 <= (i - 1) // 2 + 2 < 16:

@@ -18,9 +18,8 @@ P = 128
 NQ = 4
 NCT = 32
 NPE = 104
-CHUNK = 38
-NCHUNK = (256 - NPE) // CHUNK
-POOL_ROUND = [(2 + (NCHUNK * q + part) * 27 // 16, q, part) for q in range(NQ) for part in range(NCHUNK)]
+POOL_ROUND = [(1 + 7 * q + 2 * part, q, part) for q in range(NQ) for part in range(4)]
+POOL_ROUND[-2:] = [(NCT - 1, 3, 2), (NCT, 3, 3)]
 PE_POOL_ROUND = [(9 + k * 22 // 32, k // 8, k % 8) for k in range(8 * NQ)]
 PE_EXIT_ROUND = {q: 1 + PE_POOL_ROUND[8 * q + 7][0] for q in range(NQ)}
 S2_ROUND = {q: max(8 * q + 10, PE_EXIT_ROUND[q] + 2) for q in range(NQ)}
@@ -42,17 +41,6 @@ def tile_cin_pb_t_kernel(tc, x, x1, x2, h2, w3, b3, out_w, out_b, out):
         ps_acc = ctx.enter_context(tc.psum_pool(name="psacc", bufs=1))
         ctx.enter_context(tc.manual_schedule())
 
-        x_sb = const.tile([P, NQ, 128], BF16, name="x_sb")
-        nc.sync.dma_start(out=x_sb[:], in_=x.rearrange("(q p) f d -> p q (f d)", p=P))
-        w3_sb = const.tile([P, 2, 512], BF16, name="w3_sb")
-        nc.sync.dma_start(out=w3_sb[:], in_=w3.rearrange("(h p) f g -> p h (f g)", p=P))
-        b3_bf = const.tile([P, 2], BF16, name="b3_bf")
-        with nc.allow_non_contiguous_dma(reason="256 bias values, one per partition and half"):
-            nc.scalar.dma_start(out=b3_bf[:], in_=b3.rearrange("(h p) -> p h", p=P))
-        ow_sb = const.tile([P, 4, 128], BF16, name="ow_sb")
-        nc.scalar.dma_start(out=ow_sb[:], in_=out_w.rearrange("(t p) j -> p t j", p=P))
-        outb = const.tile([P, 128], BF16, name="outb")
-        nc.scalar.dma_start(out=outb[:], in_=out_b.partition_broadcast(P))
         h2_sb = []
         x12_sb = []
 
@@ -70,7 +58,17 @@ def tile_cin_pb_t_kernel(tc, x, x1, x2, h2, w3, b3, out_w, out_b, out):
             x12_sb.append(x12_t)
 
         load_q(0)
-
+        x_sb = const.tile([P, NQ, 128], BF16, name="x_sb")
+        nc.sync.dma_start(out=x_sb[:], in_=x.rearrange("(q p) f d -> p q (f d)", p=P))
+        w3_sb = const.tile([P, 2, 512], BF16, name="w3_sb")
+        nc.sync.dma_start(out=w3_sb[:], in_=w3.rearrange("(h p) f g -> p h (f g)", p=P))
+        b3_bf = const.tile([P, 2], BF16, name="b3_bf")
+        with nc.allow_non_contiguous_dma(reason="256 bias values, one per partition and half"):
+            nc.scalar.dma_start(out=b3_bf[:], in_=b3.rearrange("(h p) -> p h", p=P))
+        ow_sb = const.tile([P, 4, 128], BF16, name="ow_sb")
+        nc.scalar.dma_start(out=ow_sb[:], in_=out_w.rearrange("(t p) j -> p t j", p=P))
+        outb = const.tile([P, 128], BF16, name="outb")
+        nc.scalar.dma_start(out=outb[:], in_=out_b.partition_broadcast(P))
         ident_f = const.tile([P, P], F32, name="ident_f")
         make_identity(nc, ident_f[:])
         ident_b = const.tile([P, P], BF16, name="ident_b")
@@ -104,23 +102,30 @@ def tile_cin_pb_t_kernel(tc, x, x1, x2, h2, w3, b3, out_w, out_b, out):
                 load_xb(q)
             load_x12(q)
 
+        st2 = {}
         w_codes = const.tile([P, 256], U32, name="w_codes", align_bytes=64)
         w_scales = const.tile([P, 256], U8, name="w_scales", align_bytes=64)
         ow_codes = const.tile([P, 128], U32, name="ow_codes", align_bytes=64)
         ow_scales = const.tile([P, 128], U8, name="ow_scales", align_bytes=64)
 
-        def prep_w3():
+        def t_w3():
             w_t = ps_z.tile([P, 1024], BF16, name="w_t", tag="z")
             for h in range(2):
                 for f in range(4):
                     k = h * 4 + f
                     nc.tensor.transpose(w_t[:, k * P:(k + 1) * P], w3_sb[:, h, f * P:(f + 1) * P], ident_b[:])
+            st2["w_t"] = w_t
+
+        def group_w3():
             w_g = const.tile([P, 1024], BF16, name="w_g", align_bytes=64)
             nc.vector.tensor_copy(
                 out=w_g[:].rearrange("p (h o f) -> p h o f", h=2, f=4),
-                in_=w_t[:].rearrange("p (h f o) -> p h o f", h=2, f=4),
+                in_=st2["w_t"][:].rearrange("p (h f o) -> p h o f", h=2, f=4),
             )
-            nc.vector.quantize_mx(out=w_codes[:].bitcast(FP8X4), scales=w_scales[:], in_=w_g[:])
+            st2["w_g"] = w_g
+
+        def quant_w3():
+            nc.vector.quantize_mx(out=w_codes[:].bitcast(FP8X4), scales=w_scales[:], in_=st2["w_g"][:])
 
         def prep_ow():
             ow_g = const.tile([P, 512], BF16, name="ow_g", align_bytes=64)
@@ -128,7 +133,10 @@ def tile_cin_pb_t_kernel(tc, x, x1, x2, h2, w3, b3, out_w, out_b, out):
                 out=ow_g[:].rearrange("p (j t) -> p j t", t=4),
                 in_=ow_sb[:].rearrange("p t j -> p j t"),
             )
-            nc.vector.quantize_mx(out=ow_codes[:].bitcast(FP8X4), scales=ow_scales[:], in_=ow_g[:])
+            st2["ow_g"] = ow_g
+
+        def quant_ow():
+            nc.vector.quantize_mx(out=ow_codes[:].bitcast(FP8X4), scales=ow_scales[:], in_=st2["ow_g"][:])
 
         b3_f = const.tile([P, 2], F32, name="b3_f")
         nc.gpsimd.tensor_copy(out=b3_f[:], in_=b3_bf[:])
@@ -143,7 +151,6 @@ def tile_cin_pb_t_kernel(tc, x, x1, x2, h2, w3, b3, out_w, out_b, out):
         accs = {}
         pls = {}
         xps = {}
-        st2 = {}
 
         def t_h(u):
             q, b = divmod(u, 4)
@@ -280,7 +287,7 @@ def tile_cin_pb_t_kernel(tc, x, x1, x2, h2, w3, b3, out_w, out_b, out):
             if part == 0:
                 pls[q] = pl_pool.tile([P, 512], BF16, name="pl", tag="pl")
             src = x12_sb[q][:].rearrange("p (c d) -> p c d", d=32)
-            chans = slice(NPE + part * CHUNK, NPE + (part + 1) * CHUNK)
+            chans = slice(NPE + part * 38, NPE + (part + 1) * 38)
             with nc.allow_low_precision(reason="float32 sum, rounded once to bfloat16 for quantize_mx"):
                 nc.vector.tensor_reduce(out=pls[q][:, chans], in_=src[:, chans, :], axis=AX.X, op=ALU.add)
 
@@ -295,10 +302,12 @@ def tile_cin_pb_t_kernel(tc, x, x1, x2, h2, w3, b3, out_w, out_b, out):
 
         def s2_group(q):
             g2 = s2_pool.tile([P, 512], BF16, name="g2", tag="g2", align_bytes=64)
-            nc.vector.tensor_copy(
-                out=g2[:].rearrange("p (n t) -> p n t", t=4),
-                in_=st2[(q, "pt2")][:].rearrange("p (t n) -> p n t", t=4),
-            )
+            dst = g2[:].rearrange("p (n t) -> p n t", t=4)
+            src = st2[(q, "pt2")][:].rearrange("p (t n) -> p n t", t=4)
+            if q == NQ - 1:
+                nc.vector.tensor_copy(out=dst, in_=src)
+            else:
+                nc.scalar.copy(out=dst, in_=src)
             st2[(q, "g2")] = g2
 
         def s2_quant(q):
@@ -322,11 +331,12 @@ def tile_cin_pb_t_kernel(tc, x, x1, x2, h2, w3, b3, out_w, out_b, out):
             nc.sync.dma_start(out=out[q * P:(q + 1) * P, :], in_=res[:])
 
         prep_ow()
-        prep_w3()
+        quant_ow()
+        t_h(0)
         t_xb(0)
         t_xb(1)
-        t_h(0)
-        for i in range(-3, NCT + 5):
+        t_w3()
+        for i in range(-4, NCT + 5):
             q9, r9 = divmod(i - 9, 8)
             if 0 <= i - 1 < NCT:
                 relu_s(i - 1)
@@ -340,8 +350,8 @@ def tile_cin_pb_t_kernel(tc, x, x1, x2, h2, w3, b3, out_w, out_b, out):
                     s2_group(q)
             if i == 16:
                 load_xb(3)
-            if 2 <= i + 2 < 8:
-                t_xb(i + 2)
+            if 2 <= i + 3 < 8:
+                t_xb(i + 3)
             for q in range(NQ):
                 if i == S2_ROUND[q] + 1:
                     s2_mx(q)
@@ -353,8 +363,11 @@ def tile_cin_pb_t_kernel(tc, x, x1, x2, h2, w3, b3, out_w, out_b, out):
                     pe_pool(q, dg)
             if 0 <= i - 1 < NCT:
                 acc_t(i - 1)
-            if 0 <= i + 1 < NCT:
-                mult(i + 1)
+            if 0 <= i + 2 < NCT:
+                mult(i + 2)
+            if i == -1:
+                group_w3()
+                quant_w3()
             for r, q, part in POOL_ROUND:
                 if r == i:
                     pool12(q, part)
@@ -363,9 +376,8 @@ def tile_cin_pb_t_kernel(tc, x, x1, x2, h2, w3, b3, out_w, out_b, out):
                     pe_pool_exit(q)
                 if i == S2_ROUND[q]:
                     s2_quant(q)
-            if i % 2 == 0 and 0 <= i // 2 + 1 < 16:
-                hd_exit(i // 2 + 1, 1)
-            if i % 2 != 0 and 0 <= (i - 1) // 2 + 2 < 16:
-                hd_exit((i - 1) // 2 + 2, 0)
-            if i % 2 == 0 and 0 <= i // 2 + 2 < 16:
-                t_h(i // 2 + 2)
+            u, part = divmod(i + 4, 2)
+            if 0 <= u < 16:
+                hd_exit(u, part)
+            if part == 1 and u + 1 < 16:
+                t_h(u + 1)

@@ -17,12 +17,9 @@ AX = mybir.AxisListType
 P = 128
 NQ = 4
 NCT = 32
-NPE = 104
-POOL_ROUND = [(1 + 7 * q + 2 * part, q, part) for q in range(NQ) for part in range(4)]
-POOL_ROUND[-2:] = [(NCT - 1, 3, 2), (NCT, 3, 3)]
-PE_POOL_ROUND = [(9 + k * 22 // 32, k // 8, k % 8) for k in range(8 * NQ)]
-PE_EXIT_ROUND = {q: 1 + PE_POOL_ROUND[8 * q + 7][0] for q in range(NQ)}
-S2_ROUND = {q: max(8 * q + 10, PE_EXIT_ROUND[q] + 2) for q in range(NQ)}
+NPE = 103
+NXT = 32
+CHUNKS = (135, 166, 196, 226, 256)
 
 
 def tile_cin_pb_t_kernel(tc, x, x1, x2, h2, w3, b3, out_w, out_b, out):
@@ -33,10 +30,12 @@ def tile_cin_pb_t_kernel(tc, x, x1, x2, h2, w3, b3, out_w, out_b, out):
         p_pool = ctx.enter_context(tc.tile_pool(name="pp", bufs=3))
         xb_pool = ctx.enter_context(tc.tile_pool(name="xbp", bufs=2))
         y_pool = ctx.enter_context(tc.tile_pool(name="yp", bufs=4))
+        xt_pool = ctx.enter_context(tc.tile_pool(name="xtp", bufs=2))
         pl_pool = ctx.enter_context(tc.tile_pool(name="plp", bufs=4))
         s2_pool = ctx.enter_context(tc.tile_pool(name="s2p", bufs=2))
         ps_xb = ctx.enter_context(tc.psum_pool(name="psxb", bufs=4))
-        ps_z = ctx.enter_context(tc.psum_pool(name="psz", bufs=2))
+        ps_a = ctx.enter_context(tc.psum_pool(name="psa", bufs=1))
+        ps_b = ctx.enter_context(tc.psum_pool(name="psb", bufs=1))
         ps_h = ctx.enter_context(tc.psum_pool(name="psh", bufs=1))
         ps_acc = ctx.enter_context(tc.psum_pool(name="psacc", bufs=1))
         ctx.enter_context(tc.manual_schedule())
@@ -95,12 +94,22 @@ def tile_cin_pb_t_kernel(tc, x, x1, x2, h2, w3, b3, out_w, out_b, out):
             nc.sync.dma_start(out=xb_t[:], in_=x_rows(q).partition_broadcast(P))
             xbs_q[q] = xb_t
 
+        ht_sb = {}
+
+        def load_ht(q):
+            t = const.tile([P, 4096], BF16, name="ht_sb%d" % q)
+            with nc.allow_non_contiguous_dma(reason="64-byte runs: 32 positions of one sample and channel"):
+                nc.sync.dma_start(
+                    out=t[:].rearrange("g (n d) -> g n d", d=32), in_=h2[q * P:(q + 1) * P].rearrange("n g d -> g n d")
+                )
+            ht_sb[q] = t
+
         load_x12(0)
-        for q in range(1, NQ):
+        for q in (1, 2):
             load_q(q)
-            if q < 3:
-                load_xb(q)
+            load_xb(q)
             load_x12(q)
+        load_ht(3)
 
         st2 = {}
         w_codes = const.tile([P, 256], U32, name="w_codes", align_bytes=64)
@@ -109,7 +118,7 @@ def tile_cin_pb_t_kernel(tc, x, x1, x2, h2, w3, b3, out_w, out_b, out):
         ow_scales = const.tile([P, 128], U8, name="ow_scales", align_bytes=64)
 
         def t_w3():
-            w_t = ps_z.tile([P, 1024], BF16, name="w_t", tag="z")
+            w_t = ps_b.tile([P, 1024], BF16, name="w_t", tag="b")
             for h in range(2):
                 for f in range(4):
                     k = h * 4 + f
@@ -138,6 +147,10 @@ def tile_cin_pb_t_kernel(tc, x, x1, x2, h2, w3, b3, out_w, out_b, out):
         def quant_ow():
             nc.vector.quantize_mx(out=ow_codes[:].bitcast(FP8X4), scales=ow_scales[:], in_=st2["ow_g"][:])
 
+        blk = const.tile([P, 4], BF16, name="blk")
+        nc.gpsimd.memset(blk[:], 0.0)
+        for c in range(4):
+            nc.gpsimd.memset(blk[32 * c:32 * (c + 1), c:c + 1], 1.0)
         b3_f = const.tile([P, 2], F32, name="b3_f")
         nc.gpsimd.tensor_copy(out=b3_f[:], in_=b3_bf[:])
 
@@ -151,27 +164,48 @@ def tile_cin_pb_t_kernel(tc, x, x1, x2, h2, w3, b3, out_w, out_b, out):
         accs = {}
         pls = {}
         xps = {}
+        xts = {}
+        rts = {}
 
-        def t_h(u):
+        def t_h(u, halves=(0, 1)):
             q, b = divmod(u, 4)
             hw = h2_sb[q][:].bitcast(F32).rearrange("p (g j) -> p g j", j=16)
-            ht_t = ps_h.tile([P, 512], F32, name="ht_t", tag="ht")
-            for jj in range(4):
-                nc.tensor.transpose(ht_t[:, jj * P:(jj + 1) * P], hw[:, :, 4 * b + jj], ident_f[:])
-            ht[u] = ht_t
+            for half in halves:
+                if u == 0 and half == 1:
+                    ht[(u, half)] = ps_acc.tile([P, 256], F32, name="ht_b", tag="acc")
+                elif half == 0:
+                    ht_t = ps_h.tile([P, 512], F32, name="ht_t", tag="ht")
+                    ht[u] = ht_t
+                    ht[(u, 0)] = ht_t[:, 0:256]
+                    ht[(u, 1)] = ht_t[:, 256:512]
+                for jj in range(2):
+                    nc.tensor.transpose(
+                        ht[(u, half)][:, jj * P:(jj + 1) * P], hw[:, :, 4 * b + 2 * half + jj], ident_f[:]
+                    )
 
         def hd_exit(u, part):
             if part == 0:
                 hd[u] = hd_pool.tile([P, 8, 128, 2], BF16, name="hd_t", tag="hd")
-            src = ht[u][:].bitcast(BF16).rearrange("p (jj n e) -> p jj n e", jj=4, e=2)
-            dst = hd[u][:].rearrange("p (jj e) n u -> p jj e n u", e=2)
-            if u == 0:
-                pieces = [(2 * part, 2 * part + 2, e) for e in range(2)]
-            else:
-                pieces = [(0, 4, part)]
-            for lo, hi, e in pieces:
+            flat = hd[u][:].rearrange("p d n u -> p (d n u)")[:, 1024 * part:1024 * (part + 1)]
+            if u >= 12:
+                d0 = 8 * (u % 4) + 4 * part
                 nc.scalar.copy(
-                    out=dst[:, lo:hi, e, :, :], in_=src[:, lo:hi, :, e:e + 1].to_broadcast([P, hi - lo, 128, 2])
+                    out=flat.rearrange("p (n d u) -> p n d u", d=4, u=2),
+                    in_=ht_sb[3][:].rearrange("p (n d) -> p n d", d=32)[:, :, d0:d0 + 4].unsqueeze(3).to_broadcast(
+                        [P, 128, 4, 2]
+                    ),
+                )
+                return
+            if u == 0:
+                src = (ht[(u, part)] if part == 0 else ht[(u, part)][:]).bitcast(BF16).rearrange("p (jj n e) -> p jj n e", jj=2, e=2)
+                dst = flat.rearrange("p (jj e n u) -> p jj e n u", jj=2, e=2, u=2)
+                for e in range(2):
+                    nc.scalar.copy(out=dst[:, :, e, :, :], in_=src[:, :, :, e:e + 1].to_broadcast([P, 2, 128, 2]))
+            else:
+                src = ht[u][:].bitcast(BF16).rearrange("p (jj n e) -> p jj n e", jj=4, e=2)
+                dst = hd[u][:].rearrange("p (jj e) n u -> p jj e n u", e=2)
+                nc.scalar.copy(
+                    out=dst[:, :, part, :, :], in_=src[:, :, :, part:part + 1].to_broadcast([P, 4, 128, 2])
                 )
 
         def t_xb(i):
@@ -195,6 +229,17 @@ def tile_cin_pb_t_kernel(tc, x, x1, x2, h2, w3, b3, out_w, out_b, out):
             q, c = divmod(i, 8)
             if q > 0:
                 d0 = (i % 2) * 4
+                if q == 3:
+                    xv = xbs_q[q][:].bitcast(BF16).rearrange("p (n d fp e) -> p n d fp e", d=32, fp=2, e=2)
+                    hv = hd[u][:].rearrange("p d n u -> p (d n u)")[:, 256 * d0:256 * (d0 + 4)]
+                    nc.vector.tensor_tensor(
+                        out=pt[:].rearrange("p (n d fp e) -> p n d fp e", d=4, fp=2, e=2),
+                        in0=hv.rearrange("p (n d u) -> p n d u", d=4, u=2).unsqueeze(3).to_broadcast([P, 128, 4, 2, 2]),
+                        in1=xv[:, :, 4 * c:4 * c + 4],
+                        op=ALU.mult,
+                    )
+                    pts[i] = pt
+                    return
                 xv = xbs_q[q][:].bitcast(BF16).rearrange("p (n d fp e) -> p d n fp e", d=32, fp=2, e=2)
                 nc.vector.tensor_tensor(
                     out=pt[:].rearrange("p (d n fp e) -> p d n fp e", d=4, fp=2, e=2),
@@ -225,7 +270,7 @@ def tile_cin_pb_t_kernel(tc, x, x1, x2, h2, w3, b3, out_w, out_b, out):
             codes, scales = cds[i]
             for h in range(2):
                 if i < 8:
-                    z = ps_z.tile([P, 512], F32, name="z", tag="z")
+                    z = (ps_b if h else ps_a).tile([P, 512], F32, name="z", tag="b" if h else "a")
                 else:
                     z = ps_xb.tile([P, 512], F32, name="z", tag="xb")
                 nc.tensor.matmul_mx(
@@ -242,30 +287,65 @@ def tile_cin_pb_t_kernel(tc, x, x1, x2, h2, w3, b3, out_w, out_b, out):
         def relu_s(i):
             for h in range(2):
                 y = y_pool.tile([P, 512], F32, name="y", tag="y")
+                z, dst = zs[(i, h)][:], y[:]
+                if i >= 24:
+                    z = z.rearrange("p (n d) -> p d n", d=4)
+                    dst = dst.rearrange("p (d n) -> p d n", d=4)
                 if i == NCT - 1 and h == 1:
                     nc.vector.tensor_scalar(
-                        out=y[:], in0=zs[(i, h)][:], scalar1=b3_f[:, h:h + 1], scalar2=0.0, op0=ALU.add, op1=ALU.max
+                        out=dst, in0=z, scalar1=b3_f[:, h:h + 1], scalar2=0.0, op0=ALU.add, op1=ALU.max
                     )
                 else:
                     nc.scalar.activation(
-                        out=y[:], in_=zs[(i, h)][:], func=ACT.Relu, bias=b3_f[:, h:h + 1], scale=1.0
+                        out=dst, in_=z, func=ACT.Relu, bias=b3_f[:, h:h + 1], scale=1.0
                     )
                 ys[(i, h)] = y
 
-        def pe_pool(q, dg):
+        def pool_id(q, dg):
             if dg == 0:
-                xps[q] = ps_z.tile([P, 4 * NPE], F32, name="xp", tag="z")
+                xps[q] = ps_a.tile([P, 4 * NPE], F32, name="xp", tag="a")
             xv = x12_sb[q][:].rearrange("p (c dg dr) -> p c dg dr", dg=8, dr=4)
             nc.tensor.matmul(
                 out=xps[q][:], lhsT=ident_b[:], rhs=xv[:, 0:NPE, dg, :], start=(dg == 0), stop=(dg == 7)
             )
 
-        def pe_pool_exit(q):
+        def pool_id_exit(q):
             with nc.allow_low_precision(reason="float32 sum, rounded once to bfloat16 for quantize_mx"):
                 nc.vector.tensor_reduce(
-                    out=pls[q][:, 0:NPE], in_=xps[q][:].rearrange("p (c dr) -> p c dr", dr=4),
-                    axis=AX.X, op=ALU.add,
+                    out=pls[q][:, 0:NPE], in_=xps[q][:].rearrange("p (c dr) -> p c dr", dr=4), axis=AX.X, op=ALU.add
                 )
+
+        def xt_transpose(q):
+            xt = ps_b.tile([P, 1024], BF16, name="xt", tag="b")
+            first = NPE * 32
+            for k in range(8):
+                nc.tensor.transpose(
+                    xt[:, k * P:(k + 1) * P], x12_sb[q][:, first + k * P:first + (k + 1) * P], ident_b[:]
+                )
+            xts[q] = xt
+
+        def xt_exit(q):
+            xt_s = xt_pool.tile([P, 1024], BF16, name="xt_s", tag="xt")
+            nc.scalar.copy(out=xt_s[:], in_=xts[q][:])
+            xts[q] = xt_s
+
+        def xt_sum(q):
+            rt = ps_b.tile([P, NXT], F32, name="rt", tag="b")
+            for k in range(8):
+                nc.tensor.matmul(
+                    out=rt[:, 4 * k:4 * (k + 1)], lhsT=xts[q][:, k * P:(k + 1) * P], rhs=blk[:],
+                    start=True, stop=True,
+                )
+            rts[q] = rt
+
+        def xt_sum_exit(q):
+            nc.vector.tensor_copy(out=pls[q][:, NPE:NPE + NXT], in_=rts[q][:])
+
+        def pool_v(q, part):
+            src = x12_sb[q][:].rearrange("p (c d) -> p c d", d=32)
+            chans = slice(CHUNKS[part], CHUNKS[part + 1])
+            with nc.allow_low_precision(reason="float32 sum, rounded once to bfloat16 for quantize_mx"):
+                nc.vector.tensor_reduce(out=pls[q][:, chans], in_=src[:, chans, :], axis=AX.X, op=ALU.add)
 
         def acc_t(i):
             q, c = divmod(i, 8)
@@ -282,14 +362,6 @@ def tile_cin_pb_t_kernel(tc, x, x1, x2, h2, w3, b3, out_w, out_b, out):
                         stop=(c == 7 and h == 1 and dl == 3),
                         is_transpose=True,
                     )
-
-        def pool12(q, part):
-            if part == 0:
-                pls[q] = pl_pool.tile([P, 512], BF16, name="pl", tag="pl")
-            src = x12_sb[q][:].rearrange("p (c d) -> p c d", d=32)
-            chans = slice(NPE + part * 38, NPE + (part + 1) * 38)
-            with nc.allow_low_precision(reason="float32 sum, rounded once to bfloat16 for quantize_mx"):
-                nc.vector.tensor_reduce(out=pls[q][:, chans], in_=src[:, chans, :], axis=AX.X, op=ALU.add)
 
         def acc_exit(q):
             nc.scalar.copy(out=pls[q][:, 256:512], in_=accs[q][:, 0:256])
@@ -330,37 +402,60 @@ def tile_cin_pb_t_kernel(tc, x, x1, x2, h2, w3, b3, out_w, out_b, out):
             nc.vector.tensor_tensor(out=res[:], in0=st2[(q, "o2")][:], in1=outb[:], op=ALU.add)
             nc.sync.dma_start(out=out[q * P:(q + 1) * P, :], in_=res[:])
 
+        tensor_work = {}
+        vector_early = {}
+        vector_work = {}
+        scalar_work = {}
+
+        def put(table, r, fn, *args):
+            table.setdefault(r, []).append((fn, args))
+
+        last_q = NQ - 1
+        chunk_rounds = ((1, 3, 5, 7), (8, 10, 12, 14), (15, 17, 19, 21), (22, 24, NCT - 1, NCT))
+        for q in range(NQ):
+            b = 9 + 5 * q
+            put(tensor_work, b, xt_transpose, q)
+            put(scalar_work, b + 1, xt_exit, q)
+            put(tensor_work, b + 3, xt_sum, q)
+            put(vector_early, b + 4, xt_sum_exit, q)
+            for dg in range(8):
+                put(tensor_work, b + dg // 2, pool_id, q, dg)
+            put(vector_work, b + 4, pool_id_exit, q)
+            for part in range(4):
+                put(vector_work, chunk_rounds[q][part], pool_v, q, part)
+            if q != last_q:
+                r = max(b + 6, 8 * q + 10)
+                put(tensor_work, r, s2_transpose, q)
+                put(scalar_work, r, s2_group, q)
+                put(vector_early, r + 2, s2_quant, q)
+                put(tensor_work, r + 2, s2_mx, q)
+                put(vector_early, r + 3, s2_out, q)
+
         prep_ow()
         quant_ow()
-        t_h(0)
+        t_h(0, halves=(0,))
         t_xb(0)
+        t_h(0, halves=(1,))
         t_xb(1)
         t_w3()
-        for i in range(-4, NCT + 5):
+        for q in range(NQ):
+            pls[q] = pl_pool.tile([P, 512], BF16, name="pl", tag="pl")
+        for i in range(-4, NCT + 2):
             q9, r9 = divmod(i - 9, 8)
             if 0 <= i - 1 < NCT:
                 relu_s(i - 1)
-            if r9 == 0 and 0 <= q9 < NQ:
+            if r9 == 0 and 0 <= q9 < NQ - 1:
                 acc_exit(q9)
+            for fn, args in vector_early.get(i, []):
+                fn(*args)
             if 0 <= i < NCT:
                 quant(i)
-            for q in range(NQ):
-                if i == S2_ROUND[q]:
-                    s2_transpose(q)
-                    s2_group(q)
-            if i == 16:
-                load_xb(3)
             if 2 <= i + 3 < 8:
                 t_xb(i + 3)
-            for q in range(NQ):
-                if i == S2_ROUND[q] + 1:
-                    s2_mx(q)
-                    s2_out(q)
             if 0 <= i < NCT:
                 mx(i)
-            for r, q, dg in PE_POOL_ROUND:
-                if r == i:
-                    pe_pool(q, dg)
+            for fn, args in tensor_work.get(i, []):
+                fn(*args)
             if 0 <= i - 1 < NCT:
                 acc_t(i - 1)
             if 0 <= i + 2 < NCT:
@@ -368,16 +463,21 @@ def tile_cin_pb_t_kernel(tc, x, x1, x2, h2, w3, b3, out_w, out_b, out):
             if i == -1:
                 group_w3()
                 quant_w3()
-            for r, q, part in POOL_ROUND:
-                if r == i:
-                    pool12(q, part)
-            for q in range(NQ):
-                if i == PE_EXIT_ROUND[q]:
-                    pe_pool_exit(q)
-                if i == S2_ROUND[q]:
-                    s2_quant(q)
+            for fn, args in vector_work.get(i, []):
+                fn(*args)
             u, part = divmod(i + 4, 2)
             if 0 <= u < 16:
                 hd_exit(u, part)
-            if part == 1 and u + 1 < 16:
+            for fn, args in scalar_work.get(i, []):
+                fn(*args)
+            if part == 1 and u + 1 < 12:
                 t_h(u + 1)
+            if i == 14:
+                load_xb(3)
+                load_x12(3)
+        acc_exit(last_q)
+        s2_transpose(last_q)
+        s2_group(last_q)
+        s2_quant(last_q)
+        s2_mx(last_q)
+        s2_out(last_q)

from contextlib import ExitStack

import concourse.mybir as mybir
from concourse.masks import make_identity

FLOPS = 2 * 16384 * 512 * 256 + 2 * 512 * 512 * 128

F32 = mybir.dt.float32
BF16 = mybir.dt.bfloat16
U32 = mybir.dt.uint32
U8 = mybir.dt.uint8
FP8X4 = mybir.dt.float8_e4m3fn_x4
ALU = mybir.AluOpType
ACT = mybir.ActivationFunctionType
AX = mybir.AxisListType

P = 128
NQ = 4
NCT = 32
NPE = 103
NXT = 32
CHUNKS = (135, 166, 196, 226, 256)


def tile_cin_pb_t_kernel(tc, x, x1, x2, h2, w3, b3, out_w, out_b, out):
    nc = tc.nc
    with ExitStack() as ctx:
        const = ctx.enter_context(tc.tile_pool(name="const", bufs=1))
        hd_pool = ctx.enter_context(tc.tile_pool(name="hdp", bufs=3))
        p_pool = ctx.enter_context(tc.tile_pool(name="pp", bufs=3))
        xb_pool = ctx.enter_context(tc.tile_pool(name="xbp", bufs=2))
        y_pool = ctx.enter_context(tc.tile_pool(name="yp", bufs=4))
        xt_pool = ctx.enter_context(tc.tile_pool(name="xtp", bufs=2))
        pl_pool = ctx.enter_context(tc.tile_pool(name="plp", bufs=4))
        s2_pool = ctx.enter_context(tc.tile_pool(name="s2p", bufs=2))
        ps_xb = ctx.enter_context(tc.psum_pool(name="psxb", bufs=4))
        ps_a = ctx.enter_context(tc.psum_pool(name="psa", bufs=1))
        ps_b = ctx.enter_context(tc.psum_pool(name="psb", bufs=1))
        ps_h = ctx.enter_context(tc.psum_pool(name="psh", bufs=1))
        ps_acc = ctx.enter_context(tc.psum_pool(name="psacc", bufs=1))
        ctx.enter_context(tc.manual_schedule())

        h2_sb = []
        x12_sb = []

        def load_q(q):
            rows = slice(q * P, (q + 1) * P)
            h2_t = const.tile([P, 4096], BF16, name="h2_sb%d" % q)
            nc.sync.dma_start(out=h2_t[:], in_=h2[rows].rearrange("n g d -> n (g d)"))
            h2_sb.append(h2_t)

        def load_x12(q):
            rows = slice(q * P, (q + 1) * P)
            x12_t = const.tile([P, 8192], BF16, name="x12_sb%d" % q)
            nc.sync.dma_start(out=x12_t[:, 0:4096], in_=x1[rows].rearrange("n g d -> n (g d)"))
            nc.sync.dma_start(out=x12_t[:, 4096:8192], in_=x2[rows].rearrange("n g d -> n (g d)"))
            x12_sb.append(x12_t)

        load_q(0)
        x_sb = const.tile([P, NQ, 128], BF16, name="x_sb")
        nc.sync.dma_start(out=x_sb[:], in_=x.rearrange("(q p) f d -> p q (f d)", p=P))
        w3_sb = const.tile([P, 2, 512], BF16, name="w3_sb")
        nc.sync.dma_start(out=w3_sb[:], in_=w3.rearrange("(h p) f g -> p h (f g)", p=P))
        b3_bf = const.tile([P, 2], BF16, name="b3_bf")
        with nc.allow_non_contiguous_dma(reason="256 bias values, one per partition and half"):
            nc.scalar.dma_start(out=b3_bf[:], in_=b3.rearrange("(h p) -> p h", p=P))
        ow_sb = const.tile([P, 4, 128], BF16, name="ow_sb")
        nc.scalar.dma_start(out=ow_sb[:], in_=out_w.rearrange("(t p) j -> p t j", p=P))
        outb = const.tile([P, 128], BF16, name="outb")
        nc.scalar.dma_start(out=outb[:], in_=out_b.partition_broadcast(P))
        ident_f = const.tile([P, P], F32, name="ident_f")
        make_identity(nc, ident_f[:])
        ident_b = const.tile([P, P], BF16, name="ident_b")
        make_identity(nc, ident_b[:])

        xw = const.tile([P, 512], BF16, name="xw")
        nc.vector.tensor_copy(
            out=xw[:].rearrange("p (q d f) -> p q d f", q=NQ, f=4),
            in_=x_sb[:].rearrange("p q (f d) -> p q d f", f=4),
        )
        xw_words = xw[:].bitcast(F32)

        def x_rows(q):
            return out[320 + 64 * (q - 1):320 + 64 * q, :].rearrange("r w -> (r w)")

        for q in range(1, NQ):
            nc.sync.dma_start(
                out=x_rows(q).rearrange("(n w) -> n w", w=64), in_=xw_words[:, 64 * q:64 * (q + 1)]
            )
        xbs_q = {}

        def load_xb(q):
            xb_t = xb_pool.tile([P, 8192], F32, name="xb_t", tag="xbq")
            nc.sync.dma_start(out=xb_t[:], in_=x_rows(q).partition_broadcast(P))
            xbs_q[q] = xb_t

        ht_sb = {}

        def load_ht(q):
            t = const.tile([P, 4096], BF16, name="ht_sb%d" % q)
            with nc.allow_non_contiguous_dma(reason="64-byte runs: 32 positions of one sample and channel"):
                nc.sync.dma_start(
                    out=t[:].rearrange("g (n d) -> g n d", d=32), in_=h2[q * P:(q + 1) * P].rearrange("n g d -> g n d")
                )
            ht_sb[q] = t

        load_x12(0)
        for q in (1, 2):
            load_q(q)
            load_xb(q)
            load_x12(q)
        load_ht(3)

        st2 = {}
        w_codes = const.tile([P, 256], U32, name="w_codes", align_bytes=64)
        w_scales = const.tile([P, 256], U8, name="w_scales", align_bytes=64)
        ow_codes = const.tile([P, 128], U32, name="ow_codes", align_bytes=64)
        ow_scales = const.tile([P, 128], U8, name="ow_scales", align_bytes=64)

        def t_w3():
            w_t = ps_b.tile([P, 1024], BF16, name="w_t", tag="b")
            for h in range(2):
                for f in range(4):
                    k = h * 4 + f
                    nc.tensor.transpose(w_t[:, k * P:(k + 1) * P], w3_sb[:, h, f * P:(f + 1) * P], ident_b[:])
            st2["w_t"] = w_t

        def group_w3():
            w_g = const.tile([P, 1024], BF16, name="w_g", align_bytes=64)
            nc.vector.tensor_copy(
                out=w_g[:].rearrange("p (h o f) -> p h o f", h=2, f=4),
                in_=st2["w_t"][:].rearrange("p (h f o) -> p h o f", h=2, f=4),
            )
            st2["w_g"] = w_g

        def quant_w3():
            nc.vector.quantize_mx(out=w_codes[:].bitcast(FP8X4), scales=w_scales[:], in_=st2["w_g"][:])

        def prep_ow():
            ow_g = const.tile([P, 512], BF16, name="ow_g", align_bytes=64)
            nc.vector.tensor_copy(
                out=ow_g[:].rearrange("p (j t) -> p j t", t=4),
                in_=ow_sb[:].rearrange("p t j -> p j t"),
            )
            st2["ow_g"] = ow_g

        def quant_ow():
            nc.vector.quantize_mx(out=ow_codes[:].bitcast(FP8X4), scales=ow_scales[:], in_=st2["ow_g"][:])

        blk = const.tile([P, 4], BF16, name="blk")
        nc.gpsimd.memset(blk[:], 0.0)
        for c in range(4):
            nc.gpsimd.memset(blk[32 * c:32 * (c + 1), c:c + 1], 1.0)
        b3_f = const.tile([P, 2], F32, name="b3_f")
        nc.gpsimd.tensor_copy(out=b3_f[:], in_=b3_bf[:])

        ht = {}
        hd = {}
        xbs = {}
        pts = {}
        cds = {}
        zs = {}
        ys = {}
        accs = {}
        pls = {}
        xps = {}
        xts = {}
        rts = {}

        def t_h(u, halves=(0, 1)):
            q, b = divmod(u, 4)
            hw = h2_sb[q][:].bitcast(F32).rearrange("p (g j) -> p g j", j=16)
            for half in halves:
                if u == 0 and half == 1:
                    ht[(u, half)] = ps_acc.tile([P, 256], F32, name="ht_b", tag="acc")
                elif half == 0:
                    ht_t = ps_h.tile([P, 512], F32, name="ht_t", tag="ht")
                    ht[u] = ht_t
                    ht[(u, 0)] = ht_t[:, 0:256]
                    ht[(u, 1)] = ht_t[:, 256:512]
                for jj in range(2):
                    nc.tensor.transpose(
                        ht[(u, half)][:, jj * P:(jj + 1) * P], hw[:, :, 4 * b + 2 * half + jj], ident_f[:]
                    )

        def hd_exit(u, part):
            if part == 0:
                hd[u] = hd_pool.tile([P, 8, 128, 2], BF16, name="hd_t", tag="hd")
            flat = hd[u][:].rearrange("p d n u -> p (d n u)")[:, 1024 * part:1024 * (part + 1)]
            if u >= 12:
                d0 = 8 * (u % 4) + 4 * part
                nc.scalar.copy(
                    out=flat.rearrange("p (n d u) -> p n d u", d=4, u=2),
                    in_=ht_sb[3][:].rearrange("p (n d) -> p n d", d=32)[:, :, d0:d0 + 4].unsqueeze(3).to_broadcast(
                        [P, 128, 4, 2]
                    ),
                )
                return
            if u == 0:
                src = (ht[(u, part)] if part == 0 else ht[(u, part)][:]).bitcast(BF16).rearrange("p (jj n e) -> p jj n e", jj=2, e=2)
                dst = flat.rearrange("p (jj e n u) -> p jj e n u", jj=2, e=2, u=2)
                for e in range(2):
                    nc.scalar.copy(out=dst[:, :, e, :, :], in_=src[:, :, :, e:e + 1].to_broadcast([P, 2, 128, 2]))
            else:
                src = ht[u][:].bitcast(BF16).rearrange("p (jj n e) -> p jj n e", jj=4, e=2)
                dst = hd[u][:].rearrange("p (jj e) n u -> p jj e n u", e=2)
                nc.scalar.copy(
                    out=dst[:, :, part, :, :], in_=src[:, :, :, part:part + 1].to_broadcast([P, 4, 128, 2])
                )

        def t_xb(i):
            q, c = divmod(i, 8)
            tiles = []
            for s in range(2):
                xb = ps_xb.tile([P, 512], F32, name="xb", tag="xb")
                for fp in range(2):
                    for dl in range(2):
                        w = (q * 32 + 4 * c + 2 * s + dl) * 2 + fp
                        k = fp * 2 + dl
                        nc.tensor.transpose(
                            xb[:, k * P:(k + 1) * P], xw_words[:, w:w + 1].to_broadcast([P, P]), ident_f[:]
                        )
                tiles.append(xb)
            xbs[i] = tiles

        def mult(i):
            u = i // 2
            pt = p_pool.tile([P, 2048], BF16, name="pt", tag="pt", align_bytes=64)
            q, c = divmod(i, 8)
            if q > 0:
                d0 = (i % 2) * 4
                if q == 3:
                    xv = xbs_q[q][:].bitcast(BF16).rearrange("p (n d fp e) -> p n d fp e", d=32, fp=2, e=2)
                    hv = hd[u][:].rearrange("p d n u -> p (d n u)")[:, 256 * d0:256 * (d0 + 4)]
                    nc.vector.tensor_tensor(
                        out=pt[:].rearrange("p (n d fp e) -> p n d fp e", d=4, fp=2, e=2),
                        in0=hv.rearrange("p (n d u) -> p n d u", d=4, u=2).unsqueeze(3).to_broadcast([P, 128, 4, 2, 2]),
                        in1=xv[:, :, 4 * c:4 * c + 4],
                        op=ALU.mult,
                    )
                    pts[i] = pt
                    return
                xv = xbs_q[q][:].bitcast(BF16).rearrange("p (n d fp e) -> p d n fp e", d=32, fp=2, e=2)
                nc.vector.tensor_tensor(
                    out=pt[:].rearrange("p (d n fp e) -> p d n fp e", d=4, fp=2, e=2),
                    in0=hd[u][:, d0:d0 + 4, :, :].unsqueeze(3).to_broadcast([P, 4, 128, 2, 2]),
                    in1=xv[:, 4 * c:4 * c + 4],
                    op=ALU.mult,
                )
                pts[i] = pt
                return
            for s in range(2):
                dloc = (i % 2) * 4 + 2 * s
                in0 = hd[u][:, dloc:dloc + 2, :, :].rearrange("p d n u -> p (d n) u")
                nc.vector.tensor_tensor(
                    out=pt[:, s * 1024:(s + 1) * 1024].rearrange("p (c fp e) -> p c fp e", fp=2, e=2),
                    in0=in0.unsqueeze(2).to_broadcast([P, 256, 2, 2]),
                    in1=xbs[i][s][:].bitcast(BF16).rearrange("p (fp c e) -> p c fp e", fp=2, e=2),
                    op=ALU.mult,
                )
            pts[i] = pt

        def quant(i):
            codes = p_pool.tile([P, 512], U32, name="codes", tag="codes", align_bytes=64)
            scales = p_pool.tile([P, 512], U8, name="scales", tag="scales", align_bytes=64)
            nc.vector.quantize_mx(out=codes[:].bitcast(FP8X4), scales=scales[:], in_=pts[i][:])
            cds[i] = (codes, scales)

        def mx(i):
            codes, scales = cds[i]
            for h in range(2):
                if i < 8:
                    z = (ps_b if h else ps_a).tile([P, 512], F32, name="z", tag="b" if h else "a")
                else:
                    z = ps_xb.tile([P, 512], F32, name="z", tag="xb")
                nc.tensor.matmul_mx(
                    out=z[:],
                    lhsT=w_codes[:, h * P:(h + 1) * P].bitcast(FP8X4),
                    lhsT_scale=w_scales[:, h * P:(h + 1) * P],
                    rhs=codes[:].bitcast(FP8X4),
                    rhs_scale=scales[:],
                    start=True,
                    stop=True,
                )
                zs[(i, h)] = z

        def relu_s(i):
            for h in range(2):
                y = y_pool.tile([P, 512], F32, name="y", tag="y")
                z, dst = zs[(i, h)][:], y[:]
                if i >= 24:
                    z = z.rearrange("p (n d) -> p d n", d=4)
                    dst = dst.rearrange("p (d n) -> p d n", d=4)
                if i == NCT - 1 and h == 1:
                    nc.vector.tensor_scalar(
                        out=dst, in0=z, scalar1=b3_f[:, h:h + 1], scalar2=0.0, op0=ALU.add, op1=ALU.max
                    )
                else:
                    nc.scalar.activation(
                        out=dst, in_=z, func=ACT.Relu, bias=b3_f[:, h:h + 1], scale=1.0
                    )
                ys[(i, h)] = y

        def pool_id(q, dg):
            if dg == 0:
                xps[q] = ps_a.tile([P, 4 * NPE], F32, name="xp", tag="a")
            xv = x12_sb[q][:].rearrange("p (c dg dr) -> p c dg dr", dg=8, dr=4)
            nc.tensor.matmul(
                out=xps[q][:], lhsT=ident_b[:], rhs=xv[:, 0:NPE, dg, :], start=(dg == 0), stop=(dg == 7)
            )

        def pool_id_exit(q):
            with nc.allow_low_precision(reason="float32 sum, rounded once to bfloat16 for quantize_mx"):
                nc.vector.tensor_reduce(
                    out=pls[q][:, 0:NPE], in_=xps[q][:].rearrange("p (c dr) -> p c dr", dr=4), axis=AX.X, op=ALU.add
                )

        def xt_transpose(q):
            xt = ps_b.tile([P, 1024], BF16, name="xt", tag="b")
            first = NPE * 32
            for k in range(8):
                nc.tensor.transpose(
                    xt[:, k * P:(k + 1) * P], x12_sb[q][:, first + k * P:first + (k + 1) * P], ident_b[:]
                )
            xts[q] = xt

        def xt_exit(q):
            xt_s = xt_pool.tile([P, 1024], BF16, name="xt_s", tag="xt")
            nc.scalar.copy(out=xt_s[:], in_=xts[q][:])
            xts[q] = xt_s

        def xt_sum(q):
            rt = ps_b.tile([P, NXT], F32, name="rt", tag="b")
            for k in range(8):
                nc.tensor.matmul(
                    out=rt[:, 4 * k:4 * (k + 1)], lhsT=xts[q][:, k * P:(k + 1) * P], rhs=blk[:],
                    start=True, stop=True,
                )
            rts[q] = rt

        def xt_sum_exit(q):
            nc.vector.tensor_copy(out=pls[q][:, NPE:NPE + NXT], in_=rts[q][:])

        def pool_v(q, part):
            src = x12_sb[q][:].rearrange("p (c d) -> p c d", d=32)
            chans = slice(CHUNKS[part], CHUNKS[part + 1])
            with nc.allow_low_precision(reason="float32 sum, rounded once to bfloat16 for quantize_mx"):
                nc.vector.tensor_reduce(out=pls[q][:, chans], in_=src[:, chans, :], axis=AX.X, op=ALU.add)

        def acc_t(i):
            q, c = divmod(i, 8)
            if c == 0:
                accs[q] = ps_acc.tile([P, 256], F32, name="acc", tag="acc")
            acc = accs[q]
            for h in range(2):
                for dl in range(4):
                    nc.tensor.matmul(
                        out=acc[:, h * P:(h + 1) * P],
                        lhsT=ys[(i, h)][:, dl * P:(dl + 1) * P],
                        rhs=ident_f[:],
                        start=(c == 0 and h == 0 and dl == 0),
                        stop=(c == 7 and h == 1 and dl == 3),
                        is_transpose=True,
                    )

        def acc_exit(q):
            nc.scalar.copy(out=pls[q][:, 256:512], in_=accs[q][:, 0:256])

        def s2_transpose(q):
            pt2 = ps_xb.tile([P, 512], BF16, name="pt2", tag="xb")
            for t in range(4):
                nc.tensor.transpose(pt2[:, t * P:(t + 1) * P], pls[q][:, t * P:(t + 1) * P], ident_b[:])
            st2[(q, "pt2")] = pt2

        def s2_group(q):
            g2 = s2_pool.tile([P, 512], BF16, name="g2", tag="g2", align_bytes=64)
            dst = g2[:].rearrange("p (n t) -> p n t", t=4)
            src = st2[(q, "pt2")][:].rearrange("p (t n) -> p n t", t=4)
            if q == NQ - 1:
                nc.vector.tensor_copy(out=dst, in_=src)
            else:
                nc.scalar.copy(out=dst, in_=src)
            st2[(q, "g2")] = g2

        def s2_quant(q):
            c2 = s2_pool.tile([P, 128], U32, name="c2", tag="c2", align_bytes=64)
            sc2 = s2_pool.tile([P, 128], U8, name="sc2", tag="sc2", align_bytes=64)
            nc.vector.quantize_mx(out=c2[:].bitcast(FP8X4), scales=sc2[:], in_=st2[(q, "g2")][:])
            st2[(q, "c2")] = (c2, sc2)

        def s2_mx(q):
            c2, sc2 = st2[(q, "c2")]
            o2 = ps_xb.tile([P, 128], F32, name="o2", tag="xb")
            nc.tensor.matmul_mx(
                out=o2[:], lhsT=c2[:].bitcast(FP8X4), lhsT_scale=sc2[:],
                rhs=ow_codes[:].bitcast(FP8X4), rhs_scale=ow_scales[:], start=True, stop=True,
            )
            st2[(q, "o2")] = o2

        def s2_out(q):
            res = s2_pool.tile([P, 128], F32, name="res", tag="res")
            nc.vector.tensor_tensor(out=res[:], in0=st2[(q, "o2")][:], in1=outb[:], op=ALU.add)
            nc.sync.dma_start(out=out[q * P:(q + 1) * P, :], in_=res[:])

        tensor_work = {}
        vector_early = {}
        vector_work = {}
        scalar_work = {}

        def put(table, r, fn, *args):
            table.setdefault(r, []).append((fn, args))

        last_q = NQ - 1
        chunk_rounds = ((1, 3, 5, 7), (8, 10, 12, 14), (15, 17, 19, 21), (22, 24, NCT - 1, NCT))
        for q in range(NQ):
            b = 9 + 5 * q
            put(tensor_work, b, xt_transpose, q)
            put(scalar_work, b + 1, xt_exit, q)
            put(tensor_work, b + 3, xt_sum, q)
            put(vector_early, b + 4, xt_sum_exit, q)
            for dg in range(8):
                put(tensor_work, b + dg // 2, pool_id, q, dg)
            put(vector_work, b + 4, pool_id_exit, q)
            for part in range(4):
                put(vector_work, chunk_rounds[q][part], pool_v, q, part)
            if q != last_q:
                r = max(b + 6, 8 * q + 10)
                put(tensor_work, r, s2_transpose, q)
                put(scalar_work, r, s2_group, q)
                put(vector_early, r + 2, s2_quant, q)
                put(tensor_work, r + 2, s2_mx, q)
                put(vector_early, r + 3, s2_out, q)

        prep_ow()
        quant_ow()
        t_h(0, halves=(0,))
        t_xb(0)
        t_h(0, halves=(1,))
        t_xb(1)
        t_w3()
        for q in range(NQ):
            pls[q] = pl_pool.tile([P, 512], BF16, name="pl", tag="pl")
        for i in range(-4, NCT + 2):
            q9, r9 = divmod(i - 9, 8)
            if 0 <= i - 1 < NCT:
                relu_s(i - 1)
            if r9 == 0 and 0 <= q9 < NQ - 1:
                acc_exit(q9)
            for fn, args in vector_early.get(i, []):
                fn(*args)
            if 0 <= i < NCT:
                quant(i)
            if 2 <= i + 3 < 8:
                t_xb(i + 3)
            if 0 <= i < NCT:
                mx(i)
            for fn, args in tensor_work.get(i, []):
                fn(*args)
            if 0 <= i - 1 < NCT:
                acc_t(i - 1)
            if 0 <= i + 2 < NCT:
                mult(i + 2)
            if i == -1:
                group_w3()
                quant_w3()
            for fn, args in vector_work.get(i, []):
                fn(*args)
            u, part = divmod(i + 4, 2)
            if 0 <= u < 16:
                hd_exit(u, part)
            for fn, args in scalar_work.get(i, []):
                fn(*args)
            if part == 1 and u + 1 < 12:
                t_h(u + 1)
            if i == 14:
                load_xb(3)
                load_x12(3)
        acc_exit(last_q)
        s2_transpose(last_q)
        s2_group(last_q)
        s2_quant(last_q)
        s2_mx(last_q)
        s2_out(last_q)
